import numpy as np
import ml_dtypes


def mxq(x, axis, fmt="e4m3"):
    dtype, down = {"e4m3": (ml_dtypes.float8_e4m3fn, 7), "e5m2": (ml_dtypes.float8_e5m2, 14)}[fmt]
    v = np.moveaxis(np.asarray(x, np.float32).astype(ml_dtypes.bfloat16).astype(np.float64), axis, -1)
    blocks = v.reshape(v.shape[:-1] + (-1, 32))
    amax = np.abs(blocks).max(-1, keepdims=True)
    byte = np.maximum(np.where(amax > 0, np.frexp(amax)[1] - 1 + 127, 0) - down, 1)
    scale = np.exp2(byte - 127.0)
    codes = (blocks / scale).astype(np.float32).astype(dtype).astype(np.float64)
    return np.moveaxis((codes * scale).reshape(v.shape), -1, axis)


WIDE = False


def mx_kscale(k):
    if not WIDE:
        return np.ones(k)
    levels = np.array([10, -10, 5, -5, 0])
    a = np.random.permutation(np.resize(levels, k // 512 * 4)).reshape(k // 512, 4)
    idx = np.arange(k)
    return np.exp2(a[idx // 512, idx % 128 // 32])


BF16 = ml_dtypes.bfloat16


def bf(x):
    return np.asarray(x, np.float32).astype(BF16)


def f64(x):
    return np.asarray(x).astype(np.float64)


B, D, S, A, H, G = 256, 4096, 1024, 128, 512, 8
DG = D // G


def silu(v):
    return v / (1.0 + np.exp(-v))


def sigmoid(v):
    return 1.0 / (1.0 + np.exp(-v))


def setup_inputs():
    n = np.random.standard_normal
    t = mx_kscale(D)
    return {"y_dyn": bf(silu(n((B, D))) * t), "deter": bf(n((B, D))),
            "gru_W": bf(n((G, DG, 3 * DG)) * 2.0 / np.sqrt(DG) / t.reshape(G, DG)[:, :, None]), "gru_b": bf(n(3 * D) * 0.2)}


def reference(y_dyn, deter, gru_W, gru_b):
    yg = f64(y_dyn).reshape(B, G, DG).transpose(1, 0, 2)
    z = mxq(yg, 2, "e4m3") @ mxq(f64(gru_W), 1, "e4m3")
    z = z.transpose(1, 0, 2).reshape(B, 3 * D) + f64(gru_b)
    reset, cand, update = z[:, :D], z[:, D:2 * D], z[:, 2 * D:]
    reset = sigmoid(reset)
    cand = np.tanh(reset * cand)
    update = sigmoid(update - 1.0)
    return update * cand + (1.0 - update) * f64(deter)

@@ -1,0 +1,205 @@
+from contextlib import ExitStack
+
+import concourse.mybir as mybir
+from concourse.masks import make_identity
+
+F32 = mybir.dt.float32
+BF16 = mybir.dt.bfloat16
+U32 = mybir.dt.uint32
+U8 = mybir.dt.uint8
+FP8X4 = mybir.dt.float8_e4m3fn_x4
+FUNC = mybir.ActivationFunctionType
+ALU = mybir.AluOpType
+
+P = 128
+BATCH = 256
+D = 4096
+BLOCKS = 8
+K = 512
+PACK = 4
+CHUNK = 512
+STAGES = D // CHUNK
+TILES = CHUNK // P
+HALVES = BATCH // P
+AHEAD = 3
+ACT_COLS = (512, 416, 0)
+
+FLOPS = 2 * BATCH * K * 3 * K * BLOCKS
+
+
+def tile_blockgrucell_pb_kernel(tc, y_dyn, deter, gru_W, gru_b, out):
+    nc = tc.nc
+    with ExitStack() as ctx:
+        const = ctx.enter_context(tc.tile_pool(name="const", bufs=1))
+        yraw_pool = ctx.enter_context(tc.tile_pool(name="yraw", bufs=3))
+        ygrp_pool = ctx.enter_context(tc.tile_pool(name="ygrp", bufs=2))
+        wraw_pool = ctx.enter_context(tc.tile_pool(name="wraw", bufs=3 * (AHEAD + 1)))
+        wgrp_pool = ctx.enter_context(tc.tile_pool(name="wgrp", bufs=6))
+        wq_pool = ctx.enter_context(tc.tile_pool(name="wq", bufs=9))
+        det_pool = ctx.enter_context(tc.tile_pool(name="det", bufs=STAGES))
+        chain_pool = ctx.enter_context(tc.tile_pool(name="chain", bufs=4))
+        upd_pool = ctx.enter_context(tc.tile_pool(name="upd", bufs=3))
+        osb_pool = ctx.enter_context(tc.tile_pool(name="osb", bufs=3))
+        z_psum = ctx.enter_context(tc.psum_pool(name="zps", bufs=4))
+        dt_psum = ctx.enter_context(tc.psum_pool(name="dtps", bufs=2))
+        et_psum = ctx.enter_context(tc.psum_pool(name="etps", bufs=2))
+
+        ident_bf = const.tile([P, P], BF16, name="ident_bf")
+        make_identity(nc, ident_bf[:])
+        ident_f32 = const.tile([P, P], F32, name="ident_f32")
+        make_identity(nc, ident_f32[:])
+
+        y_codes = const.tile([P, BLOCKS, BATCH], U32, name="y_codes", align_bytes=64)
+        y_scales = const.tile([P, BLOCKS, BATCH], U8, name="y_scales", align_bytes=64)
+
+        n_bias = 3 * D // P
+        b_rows = const.tile([P, P], BF16, name="b_rows")
+        nc.vector.memset(b_rows[n_bias:P, :], 0.0)
+        nc.scalar.dma_start(out=b_rows[0:n_bias, :], in_=gru_b.rearrange("(j p) -> j p", p=P))
+        bias = const.tile([P, n_bias], F32, name="bias")
+
+        y_view = y_dyn.rearrange("(h b) k -> b h k", h=HALVES)
+        det_view = deter.rearrange("(h b) n -> b h n", h=HALVES)
+        out_view = out.rearrange("(h b) n -> b h n", h=HALVES)
+
+        y_raw = {}
+        w_raw = {}
+        det_sb = {}
+        y_done = set()
+
+        def load_y(g):
+            if g in y_raw or g in y_done:
+                return
+            yr = yraw_pool.tile([P, HALVES, K], BF16, name="yr")
+            nc.sync.dma_start(out=yr[:], in_=y_view[:, :, g * K:(g + 1) * K])
+            y_raw[g] = yr
+
+        def load_stage(s):
+            for part in range(3):
+                t = part * STAGES + s
+                g, c0 = t // 3, (t % 3) * CHUNK
+                wr = wraw_pool.tile([P, PACK, CHUNK], BF16, name="wr")
+                nc.sync.dma_start(
+                    out=wr[:],
+                    in_=gru_W[g, :, c0:c0 + CHUNK].rearrange("(p j) n -> p j n", j=PACK),
+                )
+                w_raw[t] = wr
+                load_y(g)
+            dsb = det_pool.tile([P, HALVES, CHUNK], BF16, name="dsb")
+            nc.sync.dma_start(out=dsb[:], in_=det_view[:, :, s * CHUNK:(s + 1) * CHUNK])
+            det_sb[s] = dsb
+
+        def prepare_y(g):
+            if g in y_done:
+                return
+            y_done.add(g)
+            yr = y_raw.pop(g)
+            xt = z_psum.tile([P, 2, BATCH], F32, name="xt", tag="z")
+            for h in range(HALVES):
+                words = yr[:, h, :].bitcast(F32).rearrange("b (p u) -> b u p", u=2)
+                for u in range(2):
+                    nc.tensor.transpose(xt[:, u, h * P:(h + 1) * P], words[:, u, :], ident_f32[:])
+            yg = ygrp_pool.tile([P, BATCH, PACK], BF16, name="yg", align_bytes=64)
+            nc.scalar.copy(out=yg[:].bitcast(F32), in_=xt[:].rearrange("p u b -> p b u"))
+            nc.vector.quantize_mx(
+                out=y_codes[:, g, :].bitcast(FP8X4),
+                scales=y_scales[:, g, :],
+                in_=yg[:].rearrange("p b t -> p (b t)"),
+            )
+
+        def regroup(copy, dst, src, c0, c1):
+            copy(
+                out=dst[:, c0:c1, :].rearrange("p (c i) t -> p c t i", i=4),
+                in_=src[:, :, c0:c1].rearrange("p t (c i) -> p c t i", i=4),
+            )
+
+        def quantise_chunk(t, part):
+            wr = w_raw.pop(t)
+            wg = wgrp_pool.tile([P, CHUNK, PACK], BF16, name="wg", align_bytes=64)
+            split = ACT_COLS[part]
+            if split > 0:
+                regroup(nc.scalar.copy, wg, wr, 0, split)
+            if split < CHUNK:
+                regroup(nc.vector.tensor_copy, wg, wr, split, CHUNK)
+            codes = wq_pool.tile([P, CHUNK], U32, name="codes", align_bytes=64)
+            scales = wq_pool.tile([P, CHUNK], U8, name="scales", align_bytes=64)
+            nc.vector.quantize_mx(
+                out=codes[:].bitcast(FP8X4),
+                scales=scales[:],
+                in_=wg[:].rearrange("p n t -> p (n t)"),
+            )
+            return codes, scales
+
+        def gate_passes(t, codes, scales):
+            g = t // 3
+            banks = []
+            for pair in range(TILES // 2):
+                zt = z_psum.tile([P, 2, BATCH], F32, name="zt", tag="z")
+                for i in range(2):
+                    cols = slice((2 * pair + i) * P, (2 * pair + i + 1) * P)
+                    nc.tensor.matmul_mx(
+                        out=zt[:, i, :],
+                        lhsT=codes[:, cols].bitcast(FP8X4),
+                        lhsT_scale=scales[:, cols],
+                        rhs=y_codes[:, g, :].bitcast(FP8X4),
+                        rhs_scale=y_scales[:, g, :],
+                        start=True,
+                        stop=True,
+                    )
+                banks.append(zt)
+            return banks
+
+        for s in range(AHEAD):
+            load_stage(s)
+
+        bt = dt_psum.tile([P, TILES, BATCH], BF16, name="bt", tag="dt")
+        nc.tensor.transpose(bt[:, 0, 0:P], b_rows[:], ident_bf[:])
+        nc.vector.tensor_copy(out=bias[:, 0:2 * D // P], in_=bt[:, 0, 0:2 * D // P])
+        nc.vector.tensor_scalar_add(out=bias[:, 2 * D // P:n_bias], in0=bt[:, 0, 2 * D // P:n_bias], scalar1=-1.0)
+
+        for s in range(STAGES):
+            if s + AHEAD < STAGES:
+                load_stage(s + AHEAD)
+            quantised = []
+            for part in range(3):
+                t = part * STAGES + s
+                prepare_y(t // 3)
+                quantised.append(quantise_chunk(t, part))
+
+            chain = chain_pool.tile([P, TILES, BATCH], F32, name="chain")
+            upd = upd_pool.tile([P, TILES, BATCH], F32, name="upd")
+
+            def bias_col(part, i):
+                j = part * (D // P) + s * TILES + i
+                return bias[:, j:j + 1]
+
+            r_banks = gate_passes(s, quantised[0][0], quantised[0][1])
+            for i in range(TILES):
+                nc.scalar.activation(out=chain[:, i, :], in_=r_banks[i // 2][:, i % 2, :], func=FUNC.Sigmoid,
+                                     bias=bias_col(0, i), scale=1.0)
+            c_banks = gate_passes(STAGES + s, quantised[1][0], quantised[1][1])
+            for i in range(TILES):
+                nc.vector.scalar_tensor_tensor(out=chain[:, i, :], in0=c_banks[i // 2][:, i % 2, :],
+                                               scalar=bias_col(1, i), in1=chain[:, i, :],
+                                               op0=ALU.add, op1=ALU.mult)
+            u_banks = gate_passes(2 * STAGES + s, quantised[2][0], quantised[2][1])
+            for i in range(TILES):
+                nc.scalar.activation(out=upd[:, i, :], in_=u_banks[i // 2][:, i % 2, :], func=FUNC.Sigmoid,
+                                     bias=bias_col(2, i), scale=1.0)
+            nc.scalar.activation(out=chain[:], in_=chain[:], func=FUNC.Tanh)
+
+            dsb = det_sb[s]
+            dt = dt_psum.tile([P, TILES, BATCH], BF16, name="dt", tag="dt")
+            for i in range(TILES):
+                for h in range(HALVES):
+                    nc.tensor.transpose(dt[:, i, h * P:(h + 1) * P], dsb[:, h, i * P:(i + 1) * P], ident_bf[:])
+            nc.vector.tensor_tensor(out=chain[:], in0=chain[:], in1=dt[:], op=ALU.subtract)
+            nc.vector.tensor_tensor(out=chain[:], in0=chain[:], in1=upd[:], op=ALU.mult)
+
+            osb = osb_pool.tile([P, HALVES, CHUNK], F32, name="osb")
+            for h in range(HALVES):
+                et = et_psum.tile([P, CHUNK], F32, name="et")
+                for i in range(TILES):
+                    nc.tensor.transpose(et[:, i * P:(i + 1) * P], chain[:, i, h * P:(h + 1) * P], ident_f32[:])
+                nc.vector.tensor_tensor(out=osb[:, h, :], in0=et[:], in1=dsb[:, h, :], op=ALU.add)
+            nc.sync.dma_start(out=out_view[:, :, s * CHUNK:(s + 1) * CHUNK], in_=osb[:])

@@ -19,10 +19,16 @@ K = 512
 PACK = 4
 CHUNK = 512
 STAGES = D // CHUNK
-TILES = CHUNK // P
+UNIT_TILES = 2
+UNIT = UNIT_TILES * P
+UNITS = CHUNK // UNIT
 HALVES = BATCH // P
 AHEAD = 3
-ACT_COLS = (512, 416, 0)
+POOL_E = True
+PE_DETER = False
+F_ON_ACT = ()
+ACT_COLS_FIRST = (176, 176, 176)
+ACT_COLS = (512, 224, 0)
 
 FLOPS = 2 * BATCH * K * 3 * K * BLOCKS
 
@@ -31,23 +37,23 @@ def tile_blockgrucell_pb_kernel(tc, y_dyn, deter, gru_W, gru_b, out):
     nc = tc.nc
     with ExitStack() as ctx:
         const = ctx.enter_context(tc.tile_pool(name="const", bufs=1))
-        yraw_pool = ctx.enter_context(tc.tile_pool(name="yraw", bufs=3))
+        yraw_pool = ctx.enter_context(tc.tile_pool(name="yraw", bufs=BLOCKS))
         ygrp_pool = ctx.enter_context(tc.tile_pool(name="ygrp", bufs=2))
         wraw_pool = ctx.enter_context(tc.tile_pool(name="wraw", bufs=3 * (AHEAD + 1)))
         wgrp_pool = ctx.enter_context(tc.tile_pool(name="wgrp", bufs=6))
-        wq_pool = ctx.enter_context(tc.tile_pool(name="wq", bufs=9))
+        wq_pool = ctx.enter_context(tc.tile_pool(name="wq", bufs=12))
         det_pool = ctx.enter_context(tc.tile_pool(name="det", bufs=STAGES))
-        chain_pool = ctx.enter_context(tc.tile_pool(name="chain", bufs=4))
-        upd_pool = ctx.enter_context(tc.tile_pool(name="upd", bufs=3))
+        chain_pool = ctx.enter_context(tc.tile_pool(name="chain", bufs=8))
+        upd_pool = ctx.enter_context(tc.tile_pool(name="upd", bufs=8))
         osb_pool = ctx.enter_context(tc.tile_pool(name="osb", bufs=3))
         z_psum = ctx.enter_context(tc.psum_pool(name="zps", bufs=4))
         dt_psum = ctx.enter_context(tc.psum_pool(name="dtps", bufs=2))
         et_psum = ctx.enter_context(tc.psum_pool(name="etps", bufs=2))
 
-        ident_bf = const.tile([P, P], BF16, name="ident_bf")
-        make_identity(nc, ident_bf[:])
         ident_f32 = const.tile([P, P], F32, name="ident_f32")
         make_identity(nc, ident_f32[:])
+        ident_bf = const.tile([P, P], BF16, name="ident_bf")
+        make_identity(nc, ident_bf[:])
 
         y_codes = const.tile([P, BLOCKS, BATCH], U32, name="y_codes", align_bytes=64)
         y_scales = const.tile([P, BLOCKS, BATCH], U8, name="y_scales", align_bytes=64)
@@ -65,14 +71,13 @@ def tile_blockgrucell_pb_kernel(tc, y_dyn, deter, gru_W, gru_b, out):
         y_raw = {}
         w_raw = {}
         det_sb = {}
+        y_seen = set()
         y_done = set()
 
-        def load_y(g):
-            if g in y_raw or g in y_done:
-                return
-            yr = yraw_pool.tile([P, HALVES, K], BF16, name="yr")
-            nc.sync.dma_start(out=yr[:], in_=y_view[:, :, g * K:(g + 1) * K])
-            y_raw[g] = yr
+        def load_det(s):
+            dsb = det_pool.tile([P, HALVES, CHUNK], BF16, name="dsb")
+            nc.sync.dma_start(out=dsb[:], in_=det_view[:, :, s * CHUNK:(s + 1) * CHUNK])
+            det_sb[s] = dsb
 
         def load_stage(s):
             for part in range(3):
@@ -84,16 +89,21 @@ def tile_blockgrucell_pb_kernel(tc, y_dyn, deter, gru_W, gru_b, out):
                     in_=gru_W[g, :, c0:c0 + CHUNK].rearrange("(p j) n -> p j n", j=PACK),
                 )
                 w_raw[t] = wr
-                load_y(g)
-            dsb = det_pool.tile([P, HALVES, CHUNK], BF16, name="dsb")
-            nc.sync.dma_start(out=dsb[:], in_=det_view[:, :, s * CHUNK:(s + 1) * CHUNK])
-            det_sb[s] = dsb
+                if g not in y_seen:
+                    y_seen.add(g)
+                    yr = yraw_pool.tile([P, HALVES, K], BF16, name="yr")
+                    nc.sync.dma_start(out=yr[:], in_=y_view[:, :, g * K:(g + 1) * K])
+                    y_raw[g] = yr
+            if s > 0:
+                load_det(s - 1)
+            if s == STAGES - 1:
+                load_det(s)
 
         def prepare_y(g):
             if g in y_done:
                 return
             y_done.add(g)
-            yr = y_raw.pop(g)
+            yr = y_raw[g]
             xt = z_psum.tile([P, 2, BATCH], F32, name="xt", tag="z")
             for h in range(HALVES):
                 words = yr[:, h, :].bitcast(F32).rearrange("b (p u) -> b u p", u=2)
@@ -113,10 +123,9 @@ def tile_blockgrucell_pb_kernel(tc, y_dyn, deter, gru_W, gru_b, out):
                 in_=src[:, :, c0:c1].rearrange("p t (c i) -> p c t i", i=4),
             )
 
-        def quantise_chunk(t, part):
-            wr = w_raw.pop(t)
+        def quantise_chunk(t, split):
+            wr = w_raw[t]
             wg = wgrp_pool.tile([P, CHUNK, PACK], BF16, name="wg", align_bytes=64)
-            split = ACT_COLS[part]
             if split > 0:
                 regroup(nc.scalar.copy, wg, wr, 0, split)
             if split < CHUNK:
@@ -130,29 +139,27 @@ def tile_blockgrucell_pb_kernel(tc, y_dyn, deter, gru_W, gru_b, out):
             )
             return codes, scales
 
-        def gate_passes(t, codes, scales):
+        def gate_passes(t, v, quantised):
+            codes, scales = quantised
             g = t // 3
-            banks = []
-            for pair in range(TILES // 2):
-                zt = z_psum.tile([P, 2, BATCH], F32, name="zt", tag="z")
-                for i in range(2):
-                    cols = slice((2 * pair + i) * P, (2 * pair + i + 1) * P)
-                    nc.tensor.matmul_mx(
-                        out=zt[:, i, :],
-                        lhsT=codes[:, cols].bitcast(FP8X4),
-                        lhsT_scale=scales[:, cols],
-                        rhs=y_codes[:, g, :].bitcast(FP8X4),
-                        rhs_scale=y_scales[:, g, :],
-                        start=True,
-                        stop=True,
-                    )
-                banks.append(zt)
-            return banks
+            zt = z_psum.tile([P, UNIT_TILES, BATCH], F32, name="zt", tag="z")
+            for i in range(UNIT_TILES):
+                cols = slice((v * UNIT_TILES + i) * P, (v * UNIT_TILES + i + 1) * P)
+                nc.tensor.matmul_mx(
+                    out=zt[:, i, :],
+                    lhsT=codes[:, cols].bitcast(FP8X4),
+                    lhsT_scale=scales[:, cols],
+                    rhs=y_codes[:, g, :].bitcast(FP8X4),
+                    rhs_scale=y_scales[:, g, :],
+                    start=True,
+                    stop=True,
+                )
+            return zt
 
         for s in range(AHEAD):
             load_stage(s)
 
-        bt = dt_psum.tile([P, TILES, BATCH], BF16, name="bt", tag="dt")
+        bt = dt_psum.tile([P, UNIT_TILES, BATCH], BF16, name="bt", tag="dt")
         nc.tensor.transpose(bt[:, 0, 0:P], b_rows[:], ident_bf[:])
         nc.vector.tensor_copy(out=bias[:, 0:2 * D // P], in_=bt[:, 0, 0:2 * D // P])
         nc.vector.tensor_scalar_add(out=bias[:, 2 * D // P:n_bias], in0=bt[:, 0, 2 * D // P:n_bias], scalar1=-1.0)
@@ -164,42 +171,65 @@ def tile_blockgrucell_pb_kernel(tc, y_dyn, deter, gru_W, gru_b, out):
             for part in range(3):
                 t = part * STAGES + s
                 prepare_y(t // 3)
-                quantised.append(quantise_chunk(t, part))
-
-            chain = chain_pool.tile([P, TILES, BATCH], F32, name="chain")
-            upd = upd_pool.tile([P, TILES, BATCH], F32, name="upd")
-
-            def bias_col(part, i):
-                j = part * (D // P) + s * TILES + i
-                return bias[:, j:j + 1]
-
-            r_banks = gate_passes(s, quantised[0][0], quantised[0][1])
-            for i in range(TILES):
-                nc.scalar.activation(out=chain[:, i, :], in_=r_banks[i // 2][:, i % 2, :], func=FUNC.Sigmoid,
-                                     bias=bias_col(0, i), scale=1.0)
-            c_banks = gate_passes(STAGES + s, quantised[1][0], quantised[1][1])
-            for i in range(TILES):
-                nc.vector.scalar_tensor_tensor(out=chain[:, i, :], in0=c_banks[i // 2][:, i % 2, :],
-                                               scalar=bias_col(1, i), in1=chain[:, i, :],
-                                               op0=ALU.add, op1=ALU.mult)
-            u_banks = gate_passes(2 * STAGES + s, quantised[2][0], quantised[2][1])
-            for i in range(TILES):
-                nc.scalar.activation(out=upd[:, i, :], in_=u_banks[i // 2][:, i % 2, :], func=FUNC.Sigmoid,
-                                     bias=bias_col(2, i), scale=1.0)
-            nc.scalar.activation(out=chain[:], in_=chain[:], func=FUNC.Tanh)
+                quantised.append(quantise_chunk(t, (ACT_COLS_FIRST if s == 0 else ACT_COLS)[part]))
 
             dsb = det_sb[s]
-            dt = dt_psum.tile([P, TILES, BATCH], BF16, name="dt", tag="dt")
-            for i in range(TILES):
-                for h in range(HALVES):
-                    nc.tensor.transpose(dt[:, i, h * P:(h + 1) * P], dsb[:, h, i * P:(i + 1) * P], ident_bf[:])
-            nc.vector.tensor_tensor(out=chain[:], in0=chain[:], in1=dt[:], op=ALU.subtract)
-            nc.vector.tensor_tensor(out=chain[:], in0=chain[:], in1=upd[:], op=ALU.mult)
-
             osb = osb_pool.tile([P, HALVES, CHUNK], F32, name="osb")
-            for h in range(HALVES):
-                et = et_psum.tile([P, CHUNK], F32, name="et")
-                for i in range(TILES):
-                    nc.tensor.transpose(et[:, i * P:(i + 1) * P], chain[:, i, h * P:(h + 1) * P], ident_f32[:])
-                nc.vector.tensor_tensor(out=osb[:, h, :], in0=et[:], in1=dsb[:, h, :], op=ALU.add)
-            nc.sync.dma_start(out=out_view[:, :, s * CHUNK:(s + 1) * CHUNK], in_=osb[:])
+            for v in range(UNITS):
+                chain = chain_pool.tile([P, UNIT_TILES, BATCH], F32, name="chain")
+                upd = upd_pool.tile([P, UNIT_TILES, BATCH], F32, name="upd")
+                ucols = slice(v * UNIT, (v + 1) * UNIT)
+
+                def bias_col(part, i):
+                    j = part * (D // P) + (s * UNITS + v) * UNIT_TILES + i
+                    return bias[:, j:j + 1]
+
+                zr = gate_passes(s, v, quantised[0])
+                for i in range(UNIT_TILES):
+                    nc.scalar.activation(out=chain[:, i, :], in_=zr[:, i, :], func=FUNC.Sigmoid,
+                                         bias=bias_col(0, i), scale=1.0)
+                zc = gate_passes(STAGES + s, v, quantised[1])
+                for i in range(UNIT_TILES):
+                    nc.vector.scalar_tensor_tensor(out=chain[:, i, :], in0=zc[:, i, :],
+                                                   scalar=bias_col(1, i), in1=chain[:, i, :],
+                                                   op0=ALU.add, op1=ALU.mult)
+                zu = gate_passes(2 * STAGES + s, v, quantised[2])
+                for i in range(UNIT_TILES):
+                    nc.scalar.activation(out=upd[:, i, :], in_=zu[:, i, :], func=FUNC.Sigmoid,
+                                         bias=bias_col(2, i), scale=1.0)
+                nc.scalar.activation(out=chain[:], in_=chain[:], func=FUNC.Tanh)
+
+                dt = dt_psum.tile([P, UNIT_TILES, BATCH], BF16, name="dt", tag="dt")
+                for i in range(UNIT_TILES):
+                    for h in range(HALVES):
+                        c0 = v * UNIT + i * P
+                        nc.tensor.transpose(dt[:, i, h * P:(h + 1) * P], dsb[:, h, c0:c0 + P], ident_bf[:])
+                nc.vector.tensor_tensor(out=chain[:], in0=chain[:], in1=dt[:], op=ALU.subtract)
+                if POOL_E:
+                    nc.gpsimd.tensor_tensor(out=chain[:], in0=chain[:], in1=upd[:], op=ALU.mult)
+                else:
+                    nc.vector.tensor_tensor(out=chain[:], in0=chain[:], in1=upd[:], op=ALU.mult)
+
+                et = et_psum.tile([P, HALVES, UNIT], F32, name="et")
+                for h in range(HALVES):
+                    for i in range(UNIT_TILES):
+                        dst = et[:, h, i * P:(i + 1) * P]
+                        if PE_DETER:
+                            c0 = v * UNIT + i * P
+                            nc.tensor.matmul(out=dst, lhsT=ident_bf[:], rhs=dsb[:, h, c0:c0 + P], start=True, stop=False)
+                            nc.tensor.matmul(out=dst, lhsT=chain[:, i, h * P:(h + 1) * P], rhs=ident_f32[:],
+                                             is_transpose=True, start=False, stop=True)
+                        else:
+                            nc.tensor.transpose(dst, chain[:, i, h * P:(h + 1) * P], ident_f32[:])
+                if PE_DETER:
+                    if (s * UNITS + v) % 2 in F_ON_ACT:
+                        nc.scalar.copy(out=osb[:, :, ucols], in_=et[:])
+                    else:
+                        nc.vector.tensor_copy(out=osb[:, :, ucols], in_=et[:])
+                else:
+                    nc.vector.tensor_tensor(out=osb[:, :, ucols], in0=et[:], in1=dsb[:, :, ucols], op=ALU.add)
+                if s == STAGES - 1:
+                    c0 = s * CHUNK + v * UNIT
+                    nc.sync.dma_start(out=out_view[:, :, c0:c0 + UNIT], in_=osb[:, :, ucols])
+            if s < STAGES - 1:
+                nc.sync.dma_start(out=out_view[:, :, s * CHUNK:(s + 1) * CHUNK], in_=osb[:])

@@ -19,16 +19,31 @@ K = 512
 PACK = 4
 CHUNK = 512
 STAGES = D // CHUNK
-UNIT_TILES = 2
-UNIT = UNIT_TILES * P
-UNITS = CHUNK // UNIT
+UNIT = 256
+TILES = UNIT // P
+N_UNITS = D // UNIT
 HALVES = BATCH // P
-AHEAD = 3
-POOL_E = True
-PE_DETER = False
-F_ON_ACT = ()
-ACT_COLS_FIRST = (176, 176, 176)
-ACT_COLS = (512, 224, 0)
+GATES = 3
+MANUAL = True
+POOL_E = False
+POOL_E_UNTIL = 14
+PE_DETER = True
+ACT_COLS = (256, 0, 0)
+
+FIRST_LOADS = (
+    ("w", 0, 0), ("y", 0), ("w", 1, 0), ("y", 2), ("w", 2, 0), ("y", 5), ("y", 3),
+    ("w", 0, 1), ("w", 1, 1), ("w", 2, 1), ("d", 0), ("y", 6),
+    ("w", 0, 2), ("w", 1, 2), ("w", 2, 2), ("d", 1), ("y", 1),
+    ("w", 0, 3), ("w", 1, 3), ("w", 2, 3), ("d", 2), ("y", 4),
+)
+LATER_LOADS = {
+    0: (("w", 0, 4), ("w", 1, 4), ("w", 2, 4), ("d", 3), ("y", 7)),
+    2: (("w", 0, 5), ("w", 1, 5), ("w", 2, 5), ("d", 4)),
+    4: (("w", 0, 6), ("w", 1, 6), ("w", 2, 6), ("d", 5)),
+    6: (("w", 0, 7), ("w", 1, 7), ("w", 2, 7), ("d", 6), ("d", 7)),
+}
+Y_TRANSPOSE_SLOT = {1: 6, 3: 1, 5: 4, 7: 7}
+Y_QUANTISE_SLOT = {2: 6, 4: 1, 6: 4, 8: 7}
 
 FLOPS = 2 * BATCH * K * 3 * K * BLOCKS
 
@@ -39,26 +54,28 @@ def tile_blockgrucell_pb_kernel(tc, y_dyn, deter, gru_W, gru_b, out):
         const = ctx.enter_context(tc.tile_pool(name="const", bufs=1))
         yraw_pool = ctx.enter_context(tc.tile_pool(name="yraw", bufs=BLOCKS))
         ygrp_pool = ctx.enter_context(tc.tile_pool(name="ygrp", bufs=2))
-        wraw_pool = ctx.enter_context(tc.tile_pool(name="wraw", bufs=3 * (AHEAD + 1)))
-        wgrp_pool = ctx.enter_context(tc.tile_pool(name="wgrp", bufs=6))
-        wq_pool = ctx.enter_context(tc.tile_pool(name="wq", bufs=12))
+        wraw_pool = ctx.enter_context(tc.tile_pool(name="wraw", bufs=12))
+        wgrp_pool = ctx.enter_context(tc.tile_pool(name="wgrp", bufs=3))
+        wq_pool = ctx.enter_context(tc.tile_pool(name="wq", bufs=3))
         det_pool = ctx.enter_context(tc.tile_pool(name="det", bufs=STAGES))
-        chain_pool = ctx.enter_context(tc.tile_pool(name="chain", bufs=8))
-        upd_pool = ctx.enter_context(tc.tile_pool(name="upd", bufs=8))
+        chain_pool = ctx.enter_context(tc.tile_pool(name="chain", bufs=4))
+        upd_pool = ctx.enter_context(tc.tile_pool(name="upd", bufs=4))
         osb_pool = ctx.enter_context(tc.tile_pool(name="osb", bufs=3))
-        z_psum = ctx.enter_context(tc.psum_pool(name="zps", bufs=4))
+        z_psum = ctx.enter_context(tc.psum_pool(name="zps", bufs=1))
         dt_psum = ctx.enter_context(tc.psum_pool(name="dtps", bufs=2))
         et_psum = ctx.enter_context(tc.psum_pool(name="etps", bufs=2))
+        if MANUAL:
+            ctx.enter_context(tc.manual_schedule())
 
-        ident_f32 = const.tile([P, P], F32, name="ident_f32")
-        make_identity(nc, ident_f32[:])
         ident_bf = const.tile([P, P], BF16, name="ident_bf")
         make_identity(nc, ident_bf[:])
+        ident_f32 = const.tile([P, P], F32, name="ident_f32")
+        make_identity(nc, ident_f32[:])
 
         y_codes = const.tile([P, BLOCKS, BATCH], U32, name="y_codes", align_bytes=64)
         y_scales = const.tile([P, BLOCKS, BATCH], U8, name="y_scales", align_bytes=64)
 
-        n_bias = 3 * D // P
+        n_bias = GATES * D // P
         b_rows = const.tile([P, P], BF16, name="b_rows")
         nc.vector.memset(b_rows[n_bias:P, :], 0.0)
         nc.scalar.dma_start(out=b_rows[0:n_bias, :], in_=gru_b.rearrange("(j p) -> j p", p=P))
@@ -68,83 +85,113 @@ def tile_blockgrucell_pb_kernel(tc, y_dyn, deter, gru_W, gru_b, out):
         det_view = deter.rearrange("(h b) n -> b h n", h=HALVES)
         out_view = out.rearrange("(h b) n -> b h n", h=HALVES)
 
-        y_raw = {}
         w_raw = {}
+        y_raw = {}
+        y_bank = {}
+        y_grp = {}
         det_sb = {}
-        y_seen = set()
-        y_done = set()
+        w_grp = {}
+        w_q = {}
+        z_bank = {}
+        chains = {}
+        upds = {}
+        det_t = {}
+        e_t = {}
+        o_sb = {}
 
-        def load_det(s):
-            dsb = det_pool.tile([P, HALVES, CHUNK], BF16, name="dsb")
-            nc.sync.dma_start(out=dsb[:], in_=det_view[:, :, s * CHUNK:(s + 1) * CHUNK])
-            det_sb[s] = dsb
+        def live(v):
+            return 0 <= v < N_UNITS
 
-        def load_stage(s):
-            for part in range(3):
-                t = part * STAGES + s
+        def block_of(gate, v):
+            return (gate * STAGES + v // 2) // 3
+
+        def load(item):
+            if item[0] == "w":
+                gate, s = item[1], item[2]
+                t = gate * STAGES + s
                 g, c0 = t // 3, (t % 3) * CHUNK
                 wr = wraw_pool.tile([P, PACK, CHUNK], BF16, name="wr")
-                nc.sync.dma_start(
-                    out=wr[:],
-                    in_=gru_W[g, :, c0:c0 + CHUNK].rearrange("(p j) n -> p j n", j=PACK),
-                )
-                w_raw[t] = wr
-                if g not in y_seen:
-                    y_seen.add(g)
-                    yr = yraw_pool.tile([P, HALVES, K], BF16, name="yr")
-                    nc.sync.dma_start(out=yr[:], in_=y_view[:, :, g * K:(g + 1) * K])
-                    y_raw[g] = yr
-            if s > 0:
-                load_det(s - 1)
-            if s == STAGES - 1:
-                load_det(s)
+                nc.sync.dma_start(out=wr[:], in_=gru_W[g, :, c0:c0 + CHUNK].rearrange("(p j) n -> p j n", j=PACK))
+                w_raw[(gate, s)] = wr
+            elif item[0] == "y":
+                g = item[1]
+                yr = yraw_pool.tile([P, HALVES, K], BF16, name="yr")
+                nc.sync.dma_start(out=yr[:], in_=y_view[:, :, g * K:(g + 1) * K])
+                y_raw[g] = yr
+            else:
+                s = item[1]
+                dsb = det_pool.tile([P, HALVES, CHUNK], BF16, name="dsb")
+                nc.sync.dma_start(out=dsb[:], in_=det_view[:, :, s * CHUNK:(s + 1) * CHUNK])
+                det_sb[s] = dsb
 
-        def prepare_y(g):
-            if g in y_done:
-                return
-            y_done.add(g)
-            yr = y_raw[g]
-            xt = z_psum.tile([P, 2, BATCH], F32, name="xt", tag="z")
+        def y_transpose(g):
+            xt = z_psum.tile([P, 2, BATCH], F32, name="xt", tag="yt")
             for h in range(HALVES):
-                words = yr[:, h, :].bitcast(F32).rearrange("b (p u) -> b u p", u=2)
+                words = y_raw[g][:, h, :].bitcast(F32).rearrange("b (p u) -> b u p", u=2)
                 for u in range(2):
                     nc.tensor.transpose(xt[:, u, h * P:(h + 1) * P], words[:, u, :], ident_f32[:])
+            y_bank[g] = xt
+
+        def y_evacuate(g):
             yg = ygrp_pool.tile([P, BATCH, PACK], BF16, name="yg", align_bytes=64)
-            nc.scalar.copy(out=yg[:].bitcast(F32), in_=xt[:].rearrange("p u b -> p b u"))
+            nc.scalar.copy(out=yg[:].bitcast(F32), in_=y_bank[g][:].rearrange("p u b -> p b u"))
+            y_grp[g] = yg
+
+        def y_quantise(g):
             nc.vector.quantize_mx(
                 out=y_codes[:, g, :].bitcast(FP8X4),
                 scales=y_scales[:, g, :],
-                in_=yg[:].rearrange("p b t -> p (b t)"),
+                in_=y_grp[g][:].rearrange("p b t -> p (b t)"),
             )
 
-        def regroup(copy, dst, src, c0, c1):
+        def act_cols(v, gate):
+            if v == 0:
+                return 0
+            if v == 1:
+                return UNIT
+            return ACT_COLS[gate]
+
+        def grouped(v, gate):
+            if (v, gate) not in w_grp:
+                w_grp[(v, gate)] = wgrp_pool.tile([P, UNIT, PACK], BF16, name="wg%d" % gate, align_bytes=64)
+            return w_grp[(v, gate)]
+
+        def regroup(copy, v, gate, c0, c1):
+            src = w_raw[(gate, v // 2)]
+            off = (v % 2) * UNIT
             copy(
-                out=dst[:, c0:c1, :].rearrange("p (c i) t -> p c t i", i=4),
-                in_=src[:, :, c0:c1].rearrange("p t (c i) -> p c t i", i=4),
+                out=grouped(v, gate)[:, c0:c1, :].rearrange("p (c i) t -> p c t i", i=4),
+                in_=src[:, :, off + c0:off + c1].rearrange("p t (c i) -> p c t i", i=4),
             )
 
-        def quantise_chunk(t, split):
-            wr = w_raw[t]
-            wg = wgrp_pool.tile([P, CHUNK, PACK], BF16, name="wg", align_bytes=64)
-            if split > 0:
-                regroup(nc.scalar.copy, wg, wr, 0, split)
-            if split < CHUNK:
-                regroup(nc.vector.tensor_copy, wg, wr, split, CHUNK)
-            codes = wq_pool.tile([P, CHUNK], U32, name="codes", align_bytes=64)
-            scales = wq_pool.tile([P, CHUNK], U8, name="scales", align_bytes=64)
+        def regroup_scalar(v, gate):
+            if live(v) and act_cols(v, gate) > 0:
+                regroup(nc.scalar.copy, v, gate, 0, act_cols(v, gate))
+
+        def regroup_vector(v, gate):
+            if live(v) and act_cols(v, gate) < UNIT:
+                regroup(nc.vector.tensor_copy, v, gate, act_cols(v, gate), UNIT)
+
+        def quantise(v, gate):
+            if not live(v):
+                return
+            codes = wq_pool.tile([P, UNIT], U32, name="codes%d" % gate, align_bytes=64)
+            scales = wq_pool.tile([P, UNIT], U8, name="scales%d" % gate, align_bytes=64)
             nc.vector.quantize_mx(
                 out=codes[:].bitcast(FP8X4),
                 scales=scales[:],
-                in_=wg[:].rearrange("p n t -> p (n t)"),
+                in_=w_grp[(v, gate)][:].rearrange("p n t -> p (n t)"),
             )
-            return codes, scales
+            w_q[(v, gate)] = (codes, scales)
 
-        def gate_passes(t, v, quantised):
-            codes, scales = quantised
-            g = t // 3
-            zt = z_psum.tile([P, UNIT_TILES, BATCH], F32, name="zt", tag="z")
-            for i in range(UNIT_TILES):
-                cols = slice((v * UNIT_TILES + i) * P, (v * UNIT_TILES + i + 1) * P)
+        def passes(v, gate):
+            if not live(v):
+                return
+            codes, scales = w_q[(v, gate)]
+            g = block_of(gate, v)
+            zt = z_psum.tile([P, TILES, BATCH], F32, name="z%d" % gate)
+            for i in range(TILES):
+                cols = slice(i * P, (i + 1) * P)
                 nc.tensor.matmul_mx(
                     out=zt[:, i, :],
                     lhsT=codes[:, cols].bitcast(FP8X4),
@@ -154,82 +201,159 @@ def tile_blockgrucell_pb_kernel(tc, y_dyn, deter, gru_W, gru_b, out):
                     start=True,
                     stop=True,
                 )
-            return zt
+            z_bank[(v, gate)] = zt
 
-        for s in range(AHEAD):
-            load_stage(s)
+        def bias_col(gate, v, i):
+            j = gate * (D // P) + v * TILES + i
+            return bias[:, j:j + 1]
 
-        bt = dt_psum.tile([P, UNIT_TILES, BATCH], BF16, name="bt", tag="dt")
-        nc.tensor.transpose(bt[:, 0, 0:P], b_rows[:], ident_bf[:])
-        nc.vector.tensor_copy(out=bias[:, 0:2 * D // P], in_=bt[:, 0, 0:2 * D // P])
-        nc.vector.tensor_scalar_add(out=bias[:, 2 * D // P:n_bias], in0=bt[:, 0, 2 * D // P:n_bias], scalar1=-1.0)
+        def reset_gate(v):
+            if not live(v):
+                return
+            chains[v] = chain_pool.tile([P, TILES, BATCH], F32, name="chain")
+            for i in range(TILES):
+                nc.scalar.activation(out=chains[v][:, i, :], in_=z_bank[(v, 0)][:, i, :], func=FUNC.Sigmoid,
+                                     bias=bias_col(0, v, i), scale=1.0)
 
-        for s in range(STAGES):
-            if s + AHEAD < STAGES:
-                load_stage(s + AHEAD)
-            quantised = []
-            for part in range(3):
-                t = part * STAGES + s
-                prepare_y(t // 3)
-                quantised.append(quantise_chunk(t, (ACT_COLS_FIRST if s == 0 else ACT_COLS)[part]))
+        def update_gate(v):
+            if not live(v):
+                return
+            upds[v] = upd_pool.tile([P, TILES, BATCH], F32, name="upd")
+            for i in range(TILES):
+                nc.scalar.activation(out=upds[v][:, i, :], in_=z_bank[(v, 2)][:, i, :], func=FUNC.Sigmoid,
+                                     bias=bias_col(2, v, i), scale=1.0)
 
-            dsb = det_sb[s]
-            osb = osb_pool.tile([P, HALVES, CHUNK], F32, name="osb")
-            for v in range(UNITS):
-                chain = chain_pool.tile([P, UNIT_TILES, BATCH], F32, name="chain")
-                upd = upd_pool.tile([P, UNIT_TILES, BATCH], F32, name="upd")
-                ucols = slice(v * UNIT, (v + 1) * UNIT)
+        def reset_times_cand(v):
+            if not live(v):
+                return
+            for i in range(TILES):
+                nc.vector.scalar_tensor_tensor(out=chains[v][:, i, :], in0=z_bank[(v, 1)][:, i, :],
+                                               scalar=bias_col(1, v, i), in1=chains[v][:, i, :],
+                                               op0=ALU.add, op1=ALU.mult)
 
-                def bias_col(part, i):
-                    j = part * (D // P) + (s * UNITS + v) * UNIT_TILES + i
-                    return bias[:, j:j + 1]
+        def cand_tanh(v):
+            if live(v):
+                nc.scalar.activation(out=chains[v][:], in_=chains[v][:], func=FUNC.Tanh)
 
-                zr = gate_passes(s, v, quantised[0])
-                for i in range(UNIT_TILES):
-                    nc.scalar.activation(out=chain[:, i, :], in_=zr[:, i, :], func=FUNC.Sigmoid,
-                                         bias=bias_col(0, i), scale=1.0)
-                zc = gate_passes(STAGES + s, v, quantised[1])
-                for i in range(UNIT_TILES):
-                    nc.vector.scalar_tensor_tensor(out=chain[:, i, :], in0=zc[:, i, :],
-                                                   scalar=bias_col(1, i), in1=chain[:, i, :],
-                                                   op0=ALU.add, op1=ALU.mult)
-                zu = gate_passes(2 * STAGES + s, v, quantised[2])
-                for i in range(UNIT_TILES):
-                    nc.scalar.activation(out=upd[:, i, :], in_=zu[:, i, :], func=FUNC.Sigmoid,
-                                         bias=bias_col(2, i), scale=1.0)
-                nc.scalar.activation(out=chain[:], in_=chain[:], func=FUNC.Tanh)
-
-                dt = dt_psum.tile([P, UNIT_TILES, BATCH], BF16, name="dt", tag="dt")
-                for i in range(UNIT_TILES):
-                    for h in range(HALVES):
-                        c0 = v * UNIT + i * P
-                        nc.tensor.transpose(dt[:, i, h * P:(h + 1) * P], dsb[:, h, c0:c0 + P], ident_bf[:])
-                nc.vector.tensor_tensor(out=chain[:], in0=chain[:], in1=dt[:], op=ALU.subtract)
-                if POOL_E:
-                    nc.gpsimd.tensor_tensor(out=chain[:], in0=chain[:], in1=upd[:], op=ALU.mult)
-                else:
-                    nc.vector.tensor_tensor(out=chain[:], in0=chain[:], in1=upd[:], op=ALU.mult)
-
-                et = et_psum.tile([P, HALVES, UNIT], F32, name="et")
+        def deter_transpose(v):
+            if not live(v):
+                return
+            dtile = dt_psum.tile([P, TILES, BATCH], BF16, name="dtile")
+            for i in range(TILES):
                 for h in range(HALVES):
-                    for i in range(UNIT_TILES):
-                        dst = et[:, h, i * P:(i + 1) * P]
-                        if PE_DETER:
-                            c0 = v * UNIT + i * P
-                            nc.tensor.matmul(out=dst, lhsT=ident_bf[:], rhs=dsb[:, h, c0:c0 + P], start=True, stop=False)
-                            nc.tensor.matmul(out=dst, lhsT=chain[:, i, h * P:(h + 1) * P], rhs=ident_f32[:],
-                                             is_transpose=True, start=False, stop=True)
-                        else:
-                            nc.tensor.transpose(dst, chain[:, i, h * P:(h + 1) * P], ident_f32[:])
-                if PE_DETER:
-                    if (s * UNITS + v) % 2 in F_ON_ACT:
-                        nc.scalar.copy(out=osb[:, :, ucols], in_=et[:])
+                    c0 = (v % 2) * UNIT + i * P
+                    nc.tensor.transpose(dtile[:, i, h * P:(h + 1) * P], det_sb[v // 2][:, h, c0:c0 + P], ident_bf[:])
+            det_t[v] = dtile
+
+        def minus_deter(v):
+            if live(v):
+                nc.vector.tensor_tensor(out=chains[v][:], in0=chains[v][:], in1=det_t[v][:], op=ALU.subtract)
+
+        def on_pool(v):
+            return POOL_E and v < POOL_E_UNTIL
+
+        def times_update(v, engine):
+            if live(v):
+                engine.tensor_tensor(out=chains[v][:], in0=chains[v][:], in1=upds[v][:], op=ALU.mult)
+
+        def back_transpose(v):
+            if not live(v):
+                return
+            et = et_psum.tile([P, HALVES, UNIT], F32, name="et")
+            for h in range(HALVES):
+                for i in range(TILES):
+                    dst = et[:, h, i * P:(i + 1) * P]
+                    if PE_DETER:
+                        c0 = (v % 2) * UNIT + i * P
+                        nc.tensor.matmul(out=dst, lhsT=ident_bf[:], rhs=det_sb[v // 2][:, h, c0:c0 + P],
+                                         start=True, stop=False)
+                        nc.tensor.matmul(out=dst, lhsT=chains[v][:, i, h * P:(h + 1) * P], rhs=ident_f32[:],
+                                         is_transpose=True, start=False, stop=True)
                     else:
-                        nc.vector.tensor_copy(out=osb[:, :, ucols], in_=et[:])
-                else:
-                    nc.vector.tensor_tensor(out=osb[:, :, ucols], in0=et[:], in1=dsb[:, :, ucols], op=ALU.add)
-                if s == STAGES - 1:
-                    c0 = s * CHUNK + v * UNIT
-                    nc.sync.dma_start(out=out_view[:, :, c0:c0 + UNIT], in_=osb[:, :, ucols])
-            if s < STAGES - 1:
-                nc.sync.dma_start(out=out_view[:, :, s * CHUNK:(s + 1) * CHUNK], in_=osb[:])
+                        nc.tensor.transpose(dst, chains[v][:, i, h * P:(h + 1) * P], ident_f32[:])
+            e_t[v] = et
+
+        def blend(v):
+            if not live(v):
+                return
+            if v % 2 == 0:
+                o_sb[v // 2] = osb_pool.tile([P, HALVES, CHUNK], F32, name="osb")
+            ucols = slice((v % 2) * UNIT, (v % 2 + 1) * UNIT)
+            if PE_DETER:
+                nc.scalar.copy(out=o_sb[v // 2][:, :, ucols], in_=e_t[v][:])
+            else:
+                nc.vector.tensor_tensor(out=o_sb[v // 2][:, :, ucols], in0=e_t[v][:], in1=det_sb[v // 2][:, :, ucols],
+                                        op=ALU.add)
+
+        def store(v):
+            if not live(v):
+                return
+            s = v // 2
+            if s == STAGES - 1:
+                ucols = slice((v % 2) * UNIT, (v % 2 + 1) * UNIT)
+                nc.sync.dma_start(out=out_view[:, :, v * UNIT:(v + 1) * UNIT], in_=o_sb[s][:, :, ucols])
+            elif v % 2 == 1:
+                nc.sync.dma_start(out=out_view[:, :, s * CHUNK:(s + 1) * CHUNK], in_=o_sb[s][:])
+
+        for item in FIRST_LOADS:
+            load(item)
+
+        bt = z_psum.tile([P, P], BF16, name="bt", tag="yt")
+        nc.tensor.transpose(bt[:], b_rows[:], ident_bf[:])
+        nc.vector.tensor_copy(out=bias[:, 0:2 * D // P], in_=bt[:, 0:2 * D // P])
+        nc.vector.tensor_scalar_add(out=bias[:, 2 * D // P:n_bias], in0=bt[:, 2 * D // P:n_bias], scalar1=-1.0)
+
+        for gate in range(GATES):
+            g = block_of(gate, 0)
+            y_transpose(g)
+            regroup_scalar(0, gate)
+            regroup_scalar(1, gate)
+            y_evacuate(g)
+            regroup_vector(0, gate)
+            regroup_vector(1, gate)
+            if gate > 0:
+                quantise(0, gate - 1)
+                quantise(1, gate - 1)
+            y_quantise(g)
+        y_transpose(3)
+        quantise(0, GATES - 1)
+        quantise(1, GATES - 1)
+        y_evacuate(3)
+        y_quantise(3)
+        for gate in range(GATES):
+            passes(0, gate)
+
+        for k in range(N_UNITS + 3):
+            for item in LATER_LOADS.get(k, ()):
+                load(item)
+            if on_pool(k - 2):
+                times_update(k - 2, nc.gpsimd)
+            reset_gate(k)
+            cand_tanh(k - 1)
+            update_gate(k)
+            if PE_DETER:
+                blend(k - 3)
+            if k in Y_QUANTISE_SLOT:
+                y_evacuate(Y_QUANTISE_SLOT[k])
+            for gate in range(GATES):
+                regroup_scalar(k + 2, gate)
+            if not on_pool(k - 2):
+                times_update(k - 2, nc.vector)
+            if not PE_DETER:
+                blend(k - 3)
+            reset_times_cand(k)
+            minus_deter(k - 1)
+            if k + 1 >= 2:
+                for gate in range(GATES):
+                    quantise(k + 1, gate)
+            for gate in range(GATES):
+                regroup_vector(k + 2, gate)
+            if k in Y_QUANTISE_SLOT:
+                y_quantise(Y_QUANTISE_SLOT[k])
+            back_transpose(k - 2)
+            if k in Y_TRANSPOSE_SLOT:
+                y_transpose(Y_TRANSPOSE_SLOT[k])
+            for gate in range(GATES):
+                passes(k + 1, gate)
+            deter_transpose(k)
+            store(k - 3)

@@ -62,7 +62,8 @@ def tile_blockgrucell_pb_kernel(tc, y_dyn, deter, gru_W, gru_b, out):
         upd_pool = ctx.enter_context(tc.tile_pool(name="upd", bufs=4))
         osb_pool = ctx.enter_context(tc.tile_pool(name="osb", bufs=3))
         z_psum = ctx.enter_context(tc.psum_pool(name="zps", bufs=1))
-        dt_psum = ctx.enter_context(tc.psum_pool(name="dtps", bufs=2))
+        dt_psum = ctx.enter_context(tc.psum_pool(name="dtps", bufs=1))
+        idle_psum = ctx.enter_context(tc.psum_pool(name="idleps", bufs=1))
         et_psum = ctx.enter_context(tc.psum_pool(name="etps", bufs=2))
         if MANUAL:
             ctx.enter_context(tc.manual_schedule())
@@ -295,6 +296,20 @@ def tile_blockgrucell_pb_kernel(tc, y_dyn, deter, gru_W, gru_b, out):
             elif v % 2 == 1:
                 nc.sync.dma_start(out=out_view[:, :, s * CHUNK:(s + 1) * CHUNK], in_=o_sb[s][:])
 
+        idle_bank = idle_psum.tile([P, 2 * BATCH], F32, name="idle_bank")
+
+        def keep_clock(n):
+            for r in range(n):
+                nc.tensor.matmul_mx(
+                    out=idle_bank[:],
+                    lhsT=y_codes[:, 2, 0:P].bitcast(FP8X4),
+                    lhsT_scale=y_scales[:, 2, 0:P],
+                    rhs=y_codes[:, 2:4, :].rearrange("p g b -> p (g b)").bitcast(FP8X4),
+                    rhs_scale=y_scales[:, 2:4, :].rearrange("p g b -> p (g b)"),
+                    start=True,
+                    stop=True,
+                )
+
         for item in FIRST_LOADS:
             load(item)
 
@@ -351,6 +366,7 @@ def tile_blockgrucell_pb_kernel(tc, y_dyn, deter, gru_W, gru_b, out):
             if k in Y_QUANTISE_SLOT:
                 y_quantise(Y_QUANTISE_SLOT[k])
             back_transpose(k - 2)
+            keep_clock(2)
             if k in Y_TRANSPOSE_SLOT:
                 y_transpose(Y_TRANSPOSE_SLOT[k])
             for gate in range(GATES):

@@ -25,10 +25,10 @@ N_UNITS = D // UNIT
 HALVES = BATCH // P
 GATES = 3
 MANUAL = True
-POOL_E = False
+POOL_E = True
 POOL_E_UNTIL = 14
 PE_DETER = True
-ACT_COLS = (256, 0, 0)
+ACT_COLS = (200, 0, 0)
 
 FIRST_LOADS = (
     ("w", 0, 0), ("y", 0), ("w", 1, 0), ("y", 2), ("w", 2, 0), ("y", 5), ("y", 3),
@@ -58,12 +58,11 @@ def tile_blockgrucell_pb_kernel(tc, y_dyn, deter, gru_W, gru_b, out):
         wgrp_pool = ctx.enter_context(tc.tile_pool(name="wgrp", bufs=3))
         wq_pool = ctx.enter_context(tc.tile_pool(name="wq", bufs=3))
         det_pool = ctx.enter_context(tc.tile_pool(name="det", bufs=STAGES))
-        chain_pool = ctx.enter_context(tc.tile_pool(name="chain", bufs=4))
+        chain_pool = ctx.enter_context(tc.tile_pool(name="chain", bufs=5))
         upd_pool = ctx.enter_context(tc.tile_pool(name="upd", bufs=4))
         osb_pool = ctx.enter_context(tc.tile_pool(name="osb", bufs=3))
         z_psum = ctx.enter_context(tc.psum_pool(name="zps", bufs=1))
-        dt_psum = ctx.enter_context(tc.psum_pool(name="dtps", bufs=1))
-        idle_psum = ctx.enter_context(tc.psum_pool(name="idleps", bufs=1))
+        dt_psum = ctx.enter_context(tc.psum_pool(name="dtps", bufs=2))
         et_psum = ctx.enter_context(tc.psum_pool(name="etps", bufs=2))
         if MANUAL:
             ctx.enter_context(tc.manual_schedule())
@@ -296,20 +295,6 @@ def tile_blockgrucell_pb_kernel(tc, y_dyn, deter, gru_W, gru_b, out):
             elif v % 2 == 1:
                 nc.sync.dma_start(out=out_view[:, :, s * CHUNK:(s + 1) * CHUNK], in_=o_sb[s][:])
 
-        idle_bank = idle_psum.tile([P, 2 * BATCH], F32, name="idle_bank")
-
-        def keep_clock(n):
-            for r in range(n):
-                nc.tensor.matmul_mx(
-                    out=idle_bank[:],
-                    lhsT=y_codes[:, 2, 0:P].bitcast(FP8X4),
-                    lhsT_scale=y_scales[:, 2, 0:P],
-                    rhs=y_codes[:, 2:4, :].rearrange("p g b -> p (g b)").bitcast(FP8X4),
-                    rhs_scale=y_scales[:, 2:4, :].rearrange("p g b -> p (g b)"),
-                    start=True,
-                    stop=True,
-                )
-
         for item in FIRST_LOADS:
             load(item)
 
@@ -338,38 +323,37 @@ def tile_blockgrucell_pb_kernel(tc, y_dyn, deter, gru_W, gru_b, out):
         for gate in range(GATES):
             passes(0, gate)
 
-        for k in range(N_UNITS + 3):
+        for k in range(N_UNITS + 4):
             for item in LATER_LOADS.get(k, ()):
                 load(item)
-            if on_pool(k - 2):
-                times_update(k - 2, nc.gpsimd)
+            if on_pool(k - 3):
+                back_transpose(k - 3)
             reset_gate(k)
-            cand_tanh(k - 1)
-            update_gate(k)
-            if PE_DETER:
-                blend(k - 3)
             if k in Y_QUANTISE_SLOT:
                 y_evacuate(Y_QUANTISE_SLOT[k])
             for gate in range(GATES):
                 regroup_scalar(k + 2, gate)
-            if not on_pool(k - 2):
-                times_update(k - 2, nc.vector)
-            if not PE_DETER:
-                blend(k - 3)
-            reset_times_cand(k)
-            minus_deter(k - 1)
+            cand_tanh(k - 1)
+            update_gate(k)
             if k + 1 >= 2:
                 for gate in range(GATES):
                     quantise(k + 1, gate)
+            if not on_pool(k - 2):
+                times_update(k - 2, nc.vector)
             for gate in range(GATES):
                 regroup_vector(k + 2, gate)
             if k in Y_QUANTISE_SLOT:
                 y_quantise(Y_QUANTISE_SLOT[k])
-            back_transpose(k - 2)
-            keep_clock(2)
+            reset_times_cand(k)
+            minus_deter(k - 1)
+            if on_pool(k - 2):
+                times_update(k - 2, nc.gpsimd)
+            if not on_pool(k - 2):
+                back_transpose(k - 2)
             if k in Y_TRANSPOSE_SLOT:
                 y_transpose(Y_TRANSPOSE_SLOT[k])
-            for gate in range(GATES):
+            for gate in (0, 2, 1):
                 passes(k + 1, gate)
             deter_transpose(k)
+            blend(k - 3)
             store(k - 3)

@@ -13,39 +13,36 @@ ALU = mybir.AluOpType
 
 P = 128
 BATCH = 256
+HALVES = BATCH // P
 D = 4096
-BLOCKS = 8
 K = 512
+BLOCKS = D // K
 PACK = 4
+R = 0
+C = 1
+U = 2
+GATES = (R, C, U)
 CHUNK = 512
 STAGES = D // CHUNK
 UNIT = 256
 TILES = UNIT // P
-N_UNITS = D // UNIT
-HALVES = BATCH // P
-GATES = 3
-MANUAL = True
-POOL_E = True
-POOL_E_UNTIL = 14
-PE_DETER = True
-ACT_COLS = (200, 0, 0)
-
-FIRST_LOADS = (
-    ("w", 0, 0), ("y", 0), ("w", 1, 0), ("y", 2), ("w", 2, 0), ("y", 5), ("y", 3),
-    ("w", 0, 1), ("w", 1, 1), ("w", 2, 1), ("d", 0), ("y", 6),
-    ("w", 0, 2), ("w", 1, 2), ("w", 2, 2), ("d", 1), ("y", 1),
-    ("w", 0, 3), ("w", 1, 3), ("w", 2, 3), ("d", 2), ("y", 4),
-)
-LATER_LOADS = {
-    0: (("w", 0, 4), ("w", 1, 4), ("w", 2, 4), ("d", 3), ("y", 7)),
-    2: (("w", 0, 5), ("w", 1, 5), ("w", 2, 5), ("d", 4)),
-    4: (("w", 0, 6), ("w", 1, 6), ("w", 2, 6), ("d", 5)),
-    6: (("w", 0, 7), ("w", 1, 7), ("w", 2, 7), ("d", 6), ("d", 7)),
-}
-Y_TRANSPOSE_SLOT = {1: 6, 3: 1, 5: 4, 7: 7}
-Y_QUANTISE_SLOT = {2: 6, 4: 1, 6: 4, 8: 7}
+UNITS = D // UNIT
+UNITS_PER_STAGE = CHUNK // UNIT
+STAGES_RESIDENT = 4
+GPSIMD_UNITS = UNITS - 2
 
 FLOPS = 2 * BATCH * K * 3 * K * BLOCKS
+
+
+def block_of(gate, stage):
+    return (gate * STAGES + stage) // 3
+
+
+def new_blocks(stage):
+    if not 0 <= stage < STAGES:
+        return []
+    seen = [block_of(gate, s) for s in range(stage) for gate in GATES]
+    return [block_of(gate, stage) for gate in GATES if block_of(gate, stage) not in seen]
 
 
 def tile_blockgrucell_pb_kernel(tc, y_dyn, deter, gru_W, gru_b, out):
@@ -54,7 +51,7 @@ def tile_blockgrucell_pb_kernel(tc, y_dyn, deter, gru_W, gru_b, out):
         const = ctx.enter_context(tc.tile_pool(name="const", bufs=1))
         yraw_pool = ctx.enter_context(tc.tile_pool(name="yraw", bufs=BLOCKS))
         ygrp_pool = ctx.enter_context(tc.tile_pool(name="ygrp", bufs=2))
-        wraw_pool = ctx.enter_context(tc.tile_pool(name="wraw", bufs=12))
+        wraw_pool = ctx.enter_context(tc.tile_pool(name="wraw", bufs=len(GATES) * STAGES_RESIDENT))
         wgrp_pool = ctx.enter_context(tc.tile_pool(name="wgrp", bufs=3))
         wq_pool = ctx.enter_context(tc.tile_pool(name="wq", bufs=3))
         det_pool = ctx.enter_context(tc.tile_pool(name="det", bufs=STAGES))
@@ -64,8 +61,7 @@ def tile_blockgrucell_pb_kernel(tc, y_dyn, deter, gru_W, gru_b, out):
         z_psum = ctx.enter_context(tc.psum_pool(name="zps", bufs=1))
         dt_psum = ctx.enter_context(tc.psum_pool(name="dtps", bufs=2))
         et_psum = ctx.enter_context(tc.psum_pool(name="etps", bufs=2))
-        if MANUAL:
-            ctx.enter_context(tc.manual_schedule())
+        ctx.enter_context(tc.manual_schedule())
 
         ident_bf = const.tile([P, P], BF16, name="ident_bf")
         make_identity(nc, ident_bf[:])
@@ -75,11 +71,11 @@ def tile_blockgrucell_pb_kernel(tc, y_dyn, deter, gru_W, gru_b, out):
         y_codes = const.tile([P, BLOCKS, BATCH], U32, name="y_codes", align_bytes=64)
         y_scales = const.tile([P, BLOCKS, BATCH], U8, name="y_scales", align_bytes=64)
 
-        n_bias = GATES * D // P
+        bias_cols = len(GATES) * D // P
         b_rows = const.tile([P, P], BF16, name="b_rows")
-        nc.vector.memset(b_rows[n_bias:P, :], 0.0)
-        nc.scalar.dma_start(out=b_rows[0:n_bias, :], in_=gru_b.rearrange("(j p) -> j p", p=P))
-        bias = const.tile([P, n_bias], F32, name="bias")
+        nc.vector.memset(b_rows[bias_cols:P, :], 0.0)
+        nc.scalar.dma_start(out=b_rows[0:bias_cols, :], in_=gru_b.rearrange("(j p) -> j p", p=P))
+        bias = const.tile([P, bias_cols], F32, name="bias")
 
         y_view = y_dyn.rearrange("(h b) k -> b h k", h=HALVES)
         det_view = deter.rearrange("(h b) n -> b h n", h=HALVES)
@@ -100,42 +96,51 @@ def tile_blockgrucell_pb_kernel(tc, y_dyn, deter, gru_W, gru_b, out):
         o_sb = {}
 
         def live(v):
-            return 0 <= v < N_UNITS
+            return 0 <= v < UNITS
 
-        def block_of(gate, v):
-            return (gate * STAGES + v // 2) // 3
+        def unit_first(v):
+            return (v % UNITS_PER_STAGE) * UNIT
 
-        def load(item):
-            if item[0] == "w":
-                gate, s = item[1], item[2]
-                t = gate * STAGES + s
-                g, c0 = t // 3, (t % 3) * CHUNK
-                wr = wraw_pool.tile([P, PACK, CHUNK], BF16, name="wr")
-                nc.sync.dma_start(out=wr[:], in_=gru_W[g, :, c0:c0 + CHUNK].rearrange("(p j) n -> p j n", j=PACK))
-                w_raw[(gate, s)] = wr
-            elif item[0] == "y":
-                g = item[1]
-                yr = yraw_pool.tile([P, HALVES, K], BF16, name="yr")
-                nc.sync.dma_start(out=yr[:], in_=y_view[:, :, g * K:(g + 1) * K])
-                y_raw[g] = yr
-            else:
-                s = item[1]
-                dsb = det_pool.tile([P, HALVES, CHUNK], BF16, name="dsb")
-                nc.sync.dma_start(out=dsb[:], in_=det_view[:, :, s * CHUNK:(s + 1) * CHUNK])
-                det_sb[s] = dsb
+        def unit_cols(v):
+            return slice(unit_first(v), unit_first(v) + UNIT)
+
+
+        def load_y(g):
+            y_raw[g] = yraw_pool.tile([P, HALVES, K], BF16, name="yr")
+            nc.sync.dma_start(out=y_raw[g][:], in_=y_view[:, :, g * K:(g + 1) * K])
+
+        def load_deter(s):
+            det_sb[s] = det_pool.tile([P, HALVES, CHUNK], BF16, name="dsb")
+            nc.sync.dma_start(out=det_sb[s][:], in_=det_view[:, :, s * CHUNK:(s + 1) * CHUNK])
+
+        def load_stage(s):
+            for gate in GATES:
+                first = ((gate * STAGES + s) % 3) * CHUNK
+                w_raw[(gate, s)] = wraw_pool.tile([P, PACK, CHUNK], BF16, name="wr")
+                nc.sync.dma_start(
+                    out=w_raw[(gate, s)][:],
+                    in_=gru_W[block_of(gate, s), :, first:first + CHUNK].rearrange("(p j) n -> p j n", j=PACK),
+                )
+                if s == 0:
+                    load_y(block_of(gate, s))
+            if s > 0:
+                load_deter(s - 1)
+            for g in new_blocks(s + 1):
+                load_y(g)
+            if s == STAGES - 1:
+                load_deter(s)
+
 
         def y_transpose(g):
-            xt = z_psum.tile([P, 2, BATCH], F32, name="xt", tag="yt")
+            y_bank[g] = z_psum.tile([P, 2, BATCH], F32, name="xt", tag="yt")
             for h in range(HALVES):
-                words = y_raw[g][:, h, :].bitcast(F32).rearrange("b (p u) -> b u p", u=2)
-                for u in range(2):
-                    nc.tensor.transpose(xt[:, u, h * P:(h + 1) * P], words[:, u, :], ident_f32[:])
-            y_bank[g] = xt
+                words = y_raw[g][:, h, :].bitcast(F32).rearrange("b (p w) -> b w p", w=2)
+                for w in range(2):
+                    nc.tensor.transpose(y_bank[g][:, w, h * P:(h + 1) * P], words[:, w, :], ident_f32[:])
 
-        def y_evacuate(g):
-            yg = ygrp_pool.tile([P, BATCH, PACK], BF16, name="yg", align_bytes=64)
-            nc.scalar.copy(out=yg[:].bitcast(F32), in_=y_bank[g][:].rearrange("p u b -> p b u"))
-            y_grp[g] = yg
+        def y_copy_out(g):
+            y_grp[g] = ygrp_pool.tile([P, BATCH, PACK], BF16, name="yg", align_bytes=64)
+            nc.scalar.copy(out=y_grp[g][:].bitcast(F32), in_=y_bank[g][:].rearrange("p w b -> p b w"))
 
         def y_quantise(g):
             nc.vector.quantize_mx(
@@ -144,33 +149,21 @@ def tile_blockgrucell_pb_kernel(tc, y_dyn, deter, gru_W, gru_b, out):
                 in_=y_grp[g][:].rearrange("p b t -> p (b t)"),
             )
 
-        def act_cols(v, gate):
-            if v == 0:
-                return 0
-            if v == 1:
-                return UNIT
-            return ACT_COLS[gate]
 
-        def grouped(v, gate):
-            if (v, gate) not in w_grp:
-                w_grp[(v, gate)] = wgrp_pool.tile([P, UNIT, PACK], BF16, name="wg%d" % gate, align_bytes=64)
-            return w_grp[(v, gate)]
+        def on_scalar(v, gate):
+            if v < UNITS_PER_STAGE:
+                return v == 1
+            return gate == R
 
-        def regroup(copy, v, gate, c0, c1):
-            src = w_raw[(gate, v // 2)]
-            off = (v % 2) * UNIT
+        def regroup(v, gate, scalar):
+            if not live(v) or on_scalar(v, gate) != scalar:
+                return
+            w_grp[(v, gate)] = wgrp_pool.tile([P, UNIT, PACK], BF16, name="wg%d" % gate, align_bytes=64)
+            copy = nc.scalar.copy if scalar else nc.vector.tensor_copy
             copy(
-                out=grouped(v, gate)[:, c0:c1, :].rearrange("p (c i) t -> p c t i", i=4),
-                in_=src[:, :, off + c0:off + c1].rearrange("p t (c i) -> p c t i", i=4),
+                out=w_grp[(v, gate)][:].rearrange("p (c i) t -> p c t i", i=4),
+                in_=w_raw[(gate, v // UNITS_PER_STAGE)][:, :, unit_cols(v)].rearrange("p t (c i) -> p c t i", i=4),
             )
-
-        def regroup_scalar(v, gate):
-            if live(v) and act_cols(v, gate) > 0:
-                regroup(nc.scalar.copy, v, gate, 0, act_cols(v, gate))
-
-        def regroup_vector(v, gate):
-            if live(v) and act_cols(v, gate) < UNIT:
-                regroup(nc.vector.tensor_copy, v, gate, act_cols(v, gate), UNIT)
 
         def quantise(v, gate):
             if not live(v):
@@ -188,12 +181,12 @@ def tile_blockgrucell_pb_kernel(tc, y_dyn, deter, gru_W, gru_b, out):
             if not live(v):
                 return
             codes, scales = w_q[(v, gate)]
-            g = block_of(gate, v)
-            zt = z_psum.tile([P, TILES, BATCH], F32, name="z%d" % gate)
+            g = block_of(gate, v // UNITS_PER_STAGE)
+            z_bank[(v, gate)] = z_psum.tile([P, TILES, BATCH], F32, name="z%d" % gate)
             for i in range(TILES):
                 cols = slice(i * P, (i + 1) * P)
                 nc.tensor.matmul_mx(
-                    out=zt[:, i, :],
+                    out=z_bank[(v, gate)][:, i, :],
                     lhsT=codes[:, cols].bitcast(FP8X4),
                     lhsT_scale=scales[:, cols],
                     rhs=y_codes[:, g, :].bitcast(FP8X4),
@@ -201,7 +194,7 @@ def tile_blockgrucell_pb_kernel(tc, y_dyn, deter, gru_W, gru_b, out):
                     start=True,
                     stop=True,
                 )
-            z_bank[(v, gate)] = zt
+
 
         def bias_col(gate, v, i):
             j = gate * (D // P) + v * TILES + i
@@ -212,23 +205,23 @@ def tile_blockgrucell_pb_kernel(tc, y_dyn, deter, gru_W, gru_b, out):
                 return
             chains[v] = chain_pool.tile([P, TILES, BATCH], F32, name="chain")
             for i in range(TILES):
-                nc.scalar.activation(out=chains[v][:, i, :], in_=z_bank[(v, 0)][:, i, :], func=FUNC.Sigmoid,
-                                     bias=bias_col(0, v, i), scale=1.0)
+                nc.scalar.activation(out=chains[v][:, i, :], in_=z_bank[(v, R)][:, i, :], func=FUNC.Sigmoid,
+                                     bias=bias_col(R, v, i), scale=1.0)
 
         def update_gate(v):
             if not live(v):
                 return
             upds[v] = upd_pool.tile([P, TILES, BATCH], F32, name="upd")
             for i in range(TILES):
-                nc.scalar.activation(out=upds[v][:, i, :], in_=z_bank[(v, 2)][:, i, :], func=FUNC.Sigmoid,
-                                     bias=bias_col(2, v, i), scale=1.0)
+                nc.scalar.activation(out=upds[v][:, i, :], in_=z_bank[(v, U)][:, i, :], func=FUNC.Sigmoid,
+                                     bias=bias_col(U, v, i), scale=1.0)
 
-        def reset_times_cand(v):
+        def reset_times_c(v):
             if not live(v):
                 return
             for i in range(TILES):
-                nc.vector.scalar_tensor_tensor(out=chains[v][:, i, :], in0=z_bank[(v, 1)][:, i, :],
-                                               scalar=bias_col(1, v, i), in1=chains[v][:, i, :],
+                nc.vector.scalar_tensor_tensor(out=chains[v][:, i, :], in0=z_bank[(v, C)][:, i, :],
+                                               scalar=bias_col(C, v, i), in1=chains[v][:, i, :],
                                                op0=ALU.add, op1=ALU.mult)
 
         def cand_tanh(v):
@@ -238,122 +231,128 @@ def tile_blockgrucell_pb_kernel(tc, y_dyn, deter, gru_W, gru_b, out):
         def deter_transpose(v):
             if not live(v):
                 return
-            dtile = dt_psum.tile([P, TILES, BATCH], BF16, name="dtile")
+            det_t[v] = dt_psum.tile([P, TILES, BATCH], BF16, name="dtile")
+            first = unit_first(v)
             for i in range(TILES):
                 for h in range(HALVES):
-                    c0 = (v % 2) * UNIT + i * P
-                    nc.tensor.transpose(dtile[:, i, h * P:(h + 1) * P], det_sb[v // 2][:, h, c0:c0 + P], ident_bf[:])
-            det_t[v] = dtile
+                    nc.tensor.transpose(det_t[v][:, i, h * P:(h + 1) * P],
+                                        det_sb[v // UNITS_PER_STAGE][:, h, first + i * P:first + (i + 1) * P],
+                                        ident_bf[:])
 
         def minus_deter(v):
             if live(v):
                 nc.vector.tensor_tensor(out=chains[v][:], in0=chains[v][:], in1=det_t[v][:], op=ALU.subtract)
 
-        def on_pool(v):
-            return POOL_E and v < POOL_E_UNTIL
+        def on_gpsimd(v):
+            return live(v) and v < GPSIMD_UNITS
 
-        def times_update(v, engine):
+        def times_update(v):
             if live(v):
+                engine = nc.gpsimd if on_gpsimd(v) else nc.vector
                 engine.tensor_tensor(out=chains[v][:], in0=chains[v][:], in1=upds[v][:], op=ALU.mult)
 
         def back_transpose(v):
             if not live(v):
                 return
-            et = et_psum.tile([P, HALVES, UNIT], F32, name="et")
+            e_t[v] = et_psum.tile([P, HALVES, UNIT], F32, name="et")
+            first = unit_first(v)
             for h in range(HALVES):
                 for i in range(TILES):
-                    dst = et[:, h, i * P:(i + 1) * P]
-                    if PE_DETER:
-                        c0 = (v % 2) * UNIT + i * P
-                        nc.tensor.matmul(out=dst, lhsT=ident_bf[:], rhs=det_sb[v // 2][:, h, c0:c0 + P],
-                                         start=True, stop=False)
-                        nc.tensor.matmul(out=dst, lhsT=chains[v][:, i, h * P:(h + 1) * P], rhs=ident_f32[:],
-                                         is_transpose=True, start=False, stop=True)
-                    else:
-                        nc.tensor.transpose(dst, chains[v][:, i, h * P:(h + 1) * P], ident_f32[:])
-            e_t[v] = et
+                    piece = e_t[v][:, h, i * P:(i + 1) * P]
+                    nc.tensor.matmul(out=piece, lhsT=ident_bf[:],
+                                     rhs=det_sb[v // UNITS_PER_STAGE][:, h, first + i * P:first + (i + 1) * P],
+                                     start=True, stop=False)
+                    nc.tensor.matmul(out=piece, lhsT=chains[v][:, i, h * P:(h + 1) * P], rhs=ident_f32[:],
+                                     is_transpose=True, start=False, stop=True)
 
-        def blend(v):
+        def copy_out(v):
             if not live(v):
                 return
-            if v % 2 == 0:
-                o_sb[v // 2] = osb_pool.tile([P, HALVES, CHUNK], F32, name="osb")
-            ucols = slice((v % 2) * UNIT, (v % 2 + 1) * UNIT)
-            if PE_DETER:
-                nc.scalar.copy(out=o_sb[v // 2][:, :, ucols], in_=e_t[v][:])
-            else:
-                nc.vector.tensor_tensor(out=o_sb[v // 2][:, :, ucols], in0=e_t[v][:], in1=det_sb[v // 2][:, :, ucols],
-                                        op=ALU.add)
+            s = v // UNITS_PER_STAGE
+            if v % UNITS_PER_STAGE == 0:
+                o_sb[s] = osb_pool.tile([P, HALVES, CHUNK], F32, name="osb")
+            nc.scalar.copy(out=o_sb[s][:, :, unit_cols(v)], in_=e_t[v][:])
 
         def store(v):
             if not live(v):
                 return
-            s = v // 2
+            s = v // UNITS_PER_STAGE
             if s == STAGES - 1:
-                ucols = slice((v % 2) * UNIT, (v % 2 + 1) * UNIT)
-                nc.sync.dma_start(out=out_view[:, :, v * UNIT:(v + 1) * UNIT], in_=o_sb[s][:, :, ucols])
-            elif v % 2 == 1:
+                nc.sync.dma_start(out=out_view[:, :, v * UNIT:(v + 1) * UNIT], in_=o_sb[s][:, :, unit_cols(v)])
+            elif v % UNITS_PER_STAGE == UNITS_PER_STAGE - 1:
                 nc.sync.dma_start(out=out_view[:, :, s * CHUNK:(s + 1) * CHUNK], in_=o_sb[s][:])
 
-        for item in FIRST_LOADS:
-            load(item)
+
+        for s in range(STAGES_RESIDENT):
+            load_stage(s)
 
         bt = z_psum.tile([P, P], BF16, name="bt", tag="yt")
         nc.tensor.transpose(bt[:], b_rows[:], ident_bf[:])
-        nc.vector.tensor_copy(out=bias[:, 0:2 * D // P], in_=bt[:, 0:2 * D // P])
-        nc.vector.tensor_scalar_add(out=bias[:, 2 * D // P:n_bias], in0=bt[:, 2 * D // P:n_bias], scalar1=-1.0)
+        u_first = U * D // P
+        nc.vector.tensor_copy(out=bias[:, 0:u_first], in_=bt[:, 0:u_first])
+        nc.vector.tensor_scalar_add(out=bias[:, u_first:bias_cols], in0=bt[:, u_first:bias_cols], scalar1=-1.0)
 
-        for gate in range(GATES):
-            g = block_of(gate, 0)
+        for gate in GATES:
+            y_transpose(block_of(gate, 0))
+            for v in range(UNITS_PER_STAGE):
+                regroup(v, gate, scalar=True)
+            y_copy_out(block_of(gate, 0))
+            for v in range(UNITS_PER_STAGE):
+                regroup(v, gate, scalar=False)
+            if gate != R:
+                for v in range(UNITS_PER_STAGE):
+                    quantise(v, gate - 1)
+            y_quantise(block_of(gate, 0))
+        for g in new_blocks(1):
             y_transpose(g)
-            regroup_scalar(0, gate)
-            regroup_scalar(1, gate)
-            y_evacuate(g)
-            regroup_vector(0, gate)
-            regroup_vector(1, gate)
-            if gate > 0:
-                quantise(0, gate - 1)
-                quantise(1, gate - 1)
+        for v in range(UNITS_PER_STAGE):
+            quantise(v, U)
+        for g in new_blocks(1):
+            y_copy_out(g)
             y_quantise(g)
-        y_transpose(3)
-        quantise(0, GATES - 1)
-        quantise(1, GATES - 1)
-        y_evacuate(3)
-        y_quantise(3)
-        for gate in range(GATES):
+        for gate in GATES:
             passes(0, gate)
 
-        for k in range(N_UNITS + 4):
-            for item in LATER_LOADS.get(k, ()):
-                load(item)
-            if on_pool(k - 3):
+        last_slot = UNITS + 3
+        for k in range(last_slot + 1):
+            if k % UNITS_PER_STAGE == 0 and k // UNITS_PER_STAGE + STAGES_RESIDENT < STAGES:
+                load_stage(k // UNITS_PER_STAGE + STAGES_RESIDENT)
+            blocks_to_transpose = new_blocks((k + 3) // UNITS_PER_STAGE) if (k + 3) % UNITS_PER_STAGE == 0 else []
+            blocks_to_quantise = new_blocks((k + 2) // UNITS_PER_STAGE) if k > 0 and k % UNITS_PER_STAGE == 0 else []
+
+            if on_gpsimd(k - 3):
                 back_transpose(k - 3)
             reset_gate(k)
-            if k in Y_QUANTISE_SLOT:
-                y_evacuate(Y_QUANTISE_SLOT[k])
-            for gate in range(GATES):
-                regroup_scalar(k + 2, gate)
+            for g in blocks_to_quantise:
+                y_copy_out(g)
+            for gate in GATES:
+                regroup(k + 2, gate, scalar=True)
             cand_tanh(k - 1)
+            if k == UNITS:
+                copy_out(k - 4)
             update_gate(k)
-            if k + 1 >= 2:
-                for gate in range(GATES):
+
+            if k > 0:
+                for gate in GATES:
                     quantise(k + 1, gate)
-            if not on_pool(k - 2):
-                times_update(k - 2, nc.vector)
-            for gate in range(GATES):
-                regroup_vector(k + 2, gate)
-            if k in Y_QUANTISE_SLOT:
-                y_quantise(Y_QUANTISE_SLOT[k])
-            reset_times_cand(k)
+            if not on_gpsimd(k - 2):
+                times_update(k - 2)
+            for gate in GATES:
+                regroup(k + 2, gate, scalar=False)
+            for g in blocks_to_quantise:
+                y_quantise(g)
+            reset_times_c(k)
             minus_deter(k - 1)
-            if on_pool(k - 2):
-                times_update(k - 2, nc.gpsimd)
-            if not on_pool(k - 2):
+
+            if on_gpsimd(k - 2):
+                times_update(k - 2)
+            else:
                 back_transpose(k - 2)
-            if k in Y_TRANSPOSE_SLOT:
-                y_transpose(Y_TRANSPOSE_SLOT[k])
-            for gate in (0, 2, 1):
+            for g in blocks_to_transpose:
+                y_transpose(g)
+            for gate in (R, U, C):
                 passes(k + 1, gate)
             deter_transpose(k)
-            blend(k - 3)
+            if k != UNITS - 1:
+                copy_out(k - 3)
             store(k - 3)

@@ -29,6 +29,7 @@ TILES = UNIT // P
 UNITS = D // UNIT
 UNITS_PER_STAGE = CHUNK // UNIT
 STAGES_RESIDENT = 4
+SCALAR_R_COLS = 224
 GPSIMD_UNITS = UNITS - 2
 
 FLOPS = 2 * BATCH * K * 3 * K * BLOCKS
@@ -150,19 +151,25 @@ def tile_blockgrucell_pb_kernel(tc, y_dyn, deter, gru_W, gru_b, out):
             )
 
 
-        def on_scalar(v, gate):
+        def scalar_cols(v, gate):
             if v < UNITS_PER_STAGE:
-                return v == 1
-            return gate == R
+                return v * UNIT
+            return SCALAR_R_COLS if gate == R else 0
 
         def regroup(v, gate, scalar):
-            if not live(v) or on_scalar(v, gate) != scalar:
+            if not live(v):
                 return
-            w_grp[(v, gate)] = wgrp_pool.tile([P, UNIT, PACK], BF16, name="wg%d" % gate, align_bytes=64)
+            split = scalar_cols(v, gate)
+            lo, hi = (0, split) if scalar else (split, UNIT)
+            if lo == hi:
+                return
+            if (v, gate) not in w_grp:
+                w_grp[(v, gate)] = wgrp_pool.tile([P, UNIT, PACK], BF16, name="wg%d" % gate, align_bytes=64)
             copy = nc.scalar.copy if scalar else nc.vector.tensor_copy
+            first = unit_first(v)
             copy(
-                out=w_grp[(v, gate)][:].rearrange("p (c i) t -> p c t i", i=4),
-                in_=w_raw[(gate, v // UNITS_PER_STAGE)][:, :, unit_cols(v)].rearrange("p t (c i) -> p c t i", i=4),
+                out=w_grp[(v, gate)][:, lo:hi, :].rearrange("p (c i) t -> p c t i", i=4),
+                in_=w_raw[(gate, v // UNITS_PER_STAGE)][:, :, first + lo:first + hi].rearrange("p t (c i) -> p c t i", i=4),
             )
 
         def quantise(v, gate):

@@ -293,12 +293,6 @@ def tile_blockgrucell_pb_kernel(tc, y_dyn, deter, gru_W, gru_b, out):
         for s in range(STAGES_RESIDENT):
             load_stage(s)
 
-        bt = z_psum.tile([P, P], BF16, name="bt", tag="yt")
-        nc.tensor.transpose(bt[:], b_rows[:], ident_bf[:])
-        u_first = U * D // P
-        nc.vector.tensor_copy(out=bias[:, 0:u_first], in_=bt[:, 0:u_first])
-        nc.vector.tensor_scalar_add(out=bias[:, u_first:bias_cols], in0=bt[:, u_first:bias_cols], scalar1=-1.0)
-
         for gate in GATES:
             y_transpose(block_of(gate, 0))
             for v in range(UNITS_PER_STAGE):
@@ -310,6 +304,11 @@ def tile_blockgrucell_pb_kernel(tc, y_dyn, deter, gru_W, gru_b, out):
                 for v in range(UNITS_PER_STAGE):
                     quantise(v, gate - 1)
             y_quantise(block_of(gate, 0))
+        bt = z_psum.tile([P, P], BF16, name="bt", tag="yt")
+        nc.tensor.transpose(bt[:], b_rows[:], ident_bf[:])
+        u_first = U * D // P
+        nc.vector.tensor_copy(out=bias[:, 0:u_first], in_=bt[:, 0:u_first])
+        nc.vector.tensor_scalar_add(out=bias[:, u_first:bias_cols], in0=bt[:, u_first:bias_cols], scalar1=-1.0)
         for g in new_blocks(1):
             y_transpose(g)
         for v in range(UNITS_PER_STAGE):

@@ -64,6 +64,11 @@ def tile_blockgrucell_pb_kernel(tc, y_dyn, deter, gru_W, gru_b, out):
         et_psum = ctx.enter_context(tc.psum_pool(name="etps", bufs=2))
         ctx.enter_context(tc.manual_schedule())
 
+        warm_in = const.tile([P, 1], F32, name="warm_in")
+        warm_out = const.tile([P, 1], F32, name="warm_out")
+        nc.vector.memset(warm_in[:], 0.0)
+        nc.scalar.activation(out=warm_out[:], in_=warm_in[:], func=FUNC.Sigmoid)
+
         ident_bf = const.tile([P, P], BF16, name="ident_bf")
         make_identity(nc, ident_bf[:])
         ident_f32 = const.tile([P, P], F32, name="ident_f32")

@@ -268,14 +268,13 @@ def tile_blockgrucell_pb_kernel(tc, y_dyn, deter, gru_W, gru_b, out):
                 return
             e_t[v] = et_psum.tile([P, HALVES, UNIT], F32, name="et")
             first = unit_first(v)
+            nc.tensor.matmul(out=e_t[v][:], lhsT=ident_bf[:], rhs=det_sb[v // UNITS_PER_STAGE][:, :, first:first + UNIT],
+                             start=True, stop=False)
             for h in range(HALVES):
                 for i in range(TILES):
-                    piece = e_t[v][:, h, i * P:(i + 1) * P]
-                    nc.tensor.matmul(out=piece, lhsT=ident_bf[:],
-                                     rhs=det_sb[v // UNITS_PER_STAGE][:, h, first + i * P:first + (i + 1) * P],
-                                     start=True, stop=False)
-                    nc.tensor.matmul(out=piece, lhsT=chains[v][:, i, h * P:(h + 1) * P], rhs=ident_f32[:],
-                                     is_transpose=True, start=False, stop=True)
+                    nc.tensor.matmul(out=e_t[v][:, h, i * P:(i + 1) * P], lhsT=chains[v][:, i, h * P:(h + 1) * P],
+                                     rhs=ident_f32[:], is_transpose=True, start=False,
+                                     stop=(h == HALVES - 1 and i == TILES - 1))
 
         def copy_out(v):
             if not live(v):

@@ -80,7 +80,9 @@ def tile_blockgrucell_pb_kernel(tc, y_dyn, deter, gru_W, gru_b, out):
         bias_cols = len(GATES) * D // P
         b_rows = const.tile([P, P], BF16, name="b_rows")
         nc.vector.memset(b_rows[bias_cols:P, :], 0.0)
-        nc.scalar.dma_start(out=b_rows[0:bias_cols, :], in_=gru_b.rearrange("(j p) -> j p", p=P))
+        b_view = gru_b.rearrange("(j p) -> j p", p=P)
+        nc.sync.dma_start(out=b_rows[0:64, :], in_=b_view[0:64, :])
+        nc.sync.dma_start(out=b_rows[64:bias_cols, :], in_=b_view[64:bias_cols, :])
         bias = const.tile([P, bias_cols], F32, name="bias")
 
         y_view = y_dyn.rearrange("(h b) k -> b h k", h=HALVES)
@@ -101,8 +103,16 @@ def tile_blockgrucell_pb_kernel(tc, y_dyn, deter, gru_W, gru_b, out):
         e_t = {}
         o_sb = {}
 
+        issued = set()
+
         def live(v):
             return 0 <= v < UNITS
+
+        def first_time(what, v, gate=None):
+            if not live(v) or (what, v, gate) in issued:
+                return False
+            issued.add((what, v, gate))
+            return True
 
         def unit_first(v):
             return (v % UNITS_PER_STAGE) * UNIT
@@ -190,7 +200,7 @@ def tile_blockgrucell_pb_kernel(tc, y_dyn, deter, gru_W, gru_b, out):
             w_q[(v, gate)] = (codes, scales)
 
         def passes(v, gate):
-            if not live(v):
+            if not first_time("passes", v, gate):
                 return
             codes, scales = w_q[(v, gate)]
             g = block_of(gate, v // UNITS_PER_STAGE)
@@ -213,7 +223,7 @@ def tile_blockgrucell_pb_kernel(tc, y_dyn, deter, gru_W, gru_b, out):
             return bias[:, j:j + 1]
 
         def reset_gate(v):
-            if not live(v):
+            if not first_time("reset", v):
                 return
             chains[v] = chain_pool.tile([P, TILES, BATCH], F32, name="chain")
             for i in range(TILES):
@@ -229,7 +239,7 @@ def tile_blockgrucell_pb_kernel(tc, y_dyn, deter, gru_W, gru_b, out):
                                      bias=bias_col(U, v, i), scale=1.0)
 
         def reset_times_c(v):
-            if not live(v):
+            if not first_time("reset times c", v):
                 return
             for i in range(TILES):
                 nc.vector.scalar_tensor_tensor(out=chains[v][:, i, :], in0=z_bank[(v, C)][:, i, :],
@@ -297,6 +307,7 @@ def tile_blockgrucell_pb_kernel(tc, y_dyn, deter, gru_W, gru_b, out):
         for s in range(STAGES_RESIDENT):
             load_stage(s)
 
+        u_first = U * D // P
         for gate in GATES:
             y_transpose(block_of(gate, 0))
             for v in range(UNITS_PER_STAGE):
@@ -307,34 +318,39 @@ def tile_blockgrucell_pb_kernel(tc, y_dyn, deter, gru_W, gru_b, out):
             if gate != R:
                 for v in range(UNITS_PER_STAGE):
                     quantise(v, gate - 1)
+            if gate == C:
+                bt = z_psum.tile([P, P], BF16, name="bt", tag="z%d" % U)
+                nc.tensor.transpose(bt[:], b_rows[:], ident_bf[:])
+                nc.vector.tensor_copy(out=bias[:, 0:u_first], in_=bt[:, 0:u_first])
+                nc.vector.tensor_scalar_add(out=bias[:, u_first:bias_cols], in0=bt[:, u_first:bias_cols], scalar1=-1.0)
             y_quantise(block_of(gate, 0))
-        bt = z_psum.tile([P, P], BF16, name="bt", tag="yt")
-        nc.tensor.transpose(bt[:], b_rows[:], ident_bf[:])
-        u_first = U * D // P
-        nc.vector.tensor_copy(out=bias[:, 0:u_first], in_=bt[:, 0:u_first])
-        nc.vector.tensor_scalar_add(out=bias[:, u_first:bias_cols], in0=bt[:, u_first:bias_cols], scalar1=-1.0)
+            if gate != R:
+                passes(0, gate - 1)
+        reset_gate(0)
         for g in new_blocks(1):
             y_transpose(g)
+        passes(1, R)
         for v in range(UNITS_PER_STAGE):
             quantise(v, U)
+        reset_times_c(0)
         for g in new_blocks(1):
             y_copy_out(g)
-            y_quantise(g)
-        for gate in GATES:
-            passes(0, gate)
+        reset_gate(1)
+        passes(0, U)
 
         last_slot = UNITS + 3
         for k in range(last_slot + 1):
             if k % UNITS_PER_STAGE == 0 and k // UNITS_PER_STAGE + STAGES_RESIDENT < STAGES:
                 load_stage(k // UNITS_PER_STAGE + STAGES_RESIDENT)
             blocks_to_transpose = new_blocks((k + 3) // UNITS_PER_STAGE) if (k + 3) % UNITS_PER_STAGE == 0 else []
-            blocks_to_quantise = new_blocks((k + 2) // UNITS_PER_STAGE) if k > 0 and k % UNITS_PER_STAGE == 0 else []
+            blocks_to_quantise = new_blocks((k + 2) // UNITS_PER_STAGE) if k % UNITS_PER_STAGE == 0 else []
 
             if on_gpsimd(k - 3):
                 back_transpose(k - 3)
             reset_gate(k)
             for g in blocks_to_quantise:
-                y_copy_out(g)
+                if k > 0:
+                    y_copy_out(g)
             for gate in GATES:
                 regroup(k + 2, gate, scalar=True)
             cand_tanh(k - 1)

@@ -183,8 +183,8 @@ def tile_blockgrucell_pb_kernel(tc, y_dyn, deter, gru_W, gru_b, out):
             copy = nc.scalar.copy if scalar else nc.vector.tensor_copy
             first = unit_first(v)
             copy(
-                out=w_grp[(v, gate)][:, lo:hi, :].rearrange("p (c i) t -> p c t i", i=4),
-                in_=w_raw[(gate, v // UNITS_PER_STAGE)][:, :, first + lo:first + hi].rearrange("p t (c i) -> p c t i", i=4),
+                out=w_grp[(v, gate)][:, lo:hi, :].rearrange("p (c i) t -> p c t i", i=8),
+                in_=w_raw[(gate, v // UNITS_PER_STAGE)][:, :, first + lo:first + hi].rearrange("p t (c i) -> p c t i", i=8),
             )
 
         def quantise(v, gate):

@@ -29,8 +29,6 @@ TILES = UNIT // P
 UNITS = D // UNIT
 UNITS_PER_STAGE = CHUNK // UNIT
 STAGES_RESIDENT = 4
-SCALAR_R_COLS = 224
-GPSIMD_UNITS = UNITS - 2
 
 FLOPS = 2 * BATCH * K * 3 * K * BLOCKS
 
@@ -54,14 +52,13 @@ def tile_blockgrucell_pb_kernel(tc, y_dyn, deter, gru_W, gru_b, out):
         ygrp_pool = ctx.enter_context(tc.tile_pool(name="ygrp", bufs=2))
         wraw_pool = ctx.enter_context(tc.tile_pool(name="wraw", bufs=len(GATES) * STAGES_RESIDENT))
         wgrp_pool = ctx.enter_context(tc.tile_pool(name="wgrp", bufs=3))
+        wgrp_u_pool = ctx.enter_context(tc.tile_pool(name="wgrpu", bufs=1))
         wq_pool = ctx.enter_context(tc.tile_pool(name="wq", bufs=3))
         det_pool = ctx.enter_context(tc.tile_pool(name="det", bufs=STAGES))
-        chain_pool = ctx.enter_context(tc.tile_pool(name="chain", bufs=5))
-        upd_pool = ctx.enter_context(tc.tile_pool(name="upd", bufs=4))
+        gate_pool = ctx.enter_context(tc.tile_pool(name="gate", bufs=4))
         osb_pool = ctx.enter_context(tc.tile_pool(name="osb", bufs=3))
         z_psum = ctx.enter_context(tc.psum_pool(name="zps", bufs=1))
-        dt_psum = ctx.enter_context(tc.psum_pool(name="dtps", bufs=2))
-        et_psum = ctx.enter_context(tc.psum_pool(name="etps", bufs=2))
+        e_psum = ctx.enter_context(tc.psum_pool(name="eps", bufs=2))
         ctx.enter_context(tc.manual_schedule())
 
         warm_in = const.tile([P, 1], F32, name="warm_in")
@@ -73,6 +70,8 @@ def tile_blockgrucell_pb_kernel(tc, y_dyn, deter, gru_W, gru_b, out):
         make_identity(nc, ident_bf[:])
         ident_f32 = const.tile([P, P], F32, name="ident_f32")
         make_identity(nc, ident_f32[:])
+        minus_ident = const.tile([P, P], BF16, name="minus_ident")
+        nc.vector.tensor_scalar_mul(out=minus_ident[:], in0=ident_bf[:], scalar1=-1.0)
 
         y_codes = const.tile([P, BLOCKS, BATCH], U32, name="y_codes", align_bytes=64)
         y_scales = const.tile([P, BLOCKS, BATCH], U8, name="y_scales", align_bytes=64)
@@ -97,10 +96,13 @@ def tile_blockgrucell_pb_kernel(tc, y_dyn, deter, gru_W, gru_b, out):
         w_grp = {}
         w_q = {}
         z_bank = {}
-        chains = {}
+        xs = {}
+        x_bank = {}
+        cands = {}
         upds = {}
-        det_t = {}
-        e_t = {}
+        diff_bank = {}
+        es = {}
+        e_bank = {}
         o_sb = {}
 
         issued = set()
@@ -148,7 +150,7 @@ def tile_blockgrucell_pb_kernel(tc, y_dyn, deter, gru_W, gru_b, out):
 
 
         def y_transpose(g):
-            y_bank[g] = z_psum.tile([P, 2, BATCH], F32, name="xt", tag="yt")
+            y_bank[g] = z_psum.tile([P, 2, BATCH], F32, name="yt")
             for h in range(HALVES):
                 words = y_raw[g][:, h, :].bitcast(F32).rearrange("b (p w) -> b w p", w=2)
                 for w in range(2):
@@ -166,25 +168,23 @@ def tile_blockgrucell_pb_kernel(tc, y_dyn, deter, gru_W, gru_b, out):
             )
 
 
-        def scalar_cols(v, gate):
-            if v < UNITS_PER_STAGE:
-                return v * UNIT
-            return SCALAR_R_COLS if gate == R else 0
-
-        def regroup(v, gate, scalar):
+        def regroup(v, gate, engine):
             if not live(v):
                 return
-            split = scalar_cols(v, gate)
-            lo, hi = (0, split) if scalar else (split, UNIT)
-            if lo == hi:
-                return
-            if (v, gate) not in w_grp:
+            if gate == U and v >= UNITS_PER_STAGE:
+                w_grp[(v, gate)] = wgrp_u_pool.tile([P, UNIT, PACK], BF16, name="wgu", align_bytes=64)
+            else:
                 w_grp[(v, gate)] = wgrp_pool.tile([P, UNIT, PACK], BF16, name="wg%d" % gate, align_bytes=64)
-            copy = nc.scalar.copy if scalar else nc.vector.tensor_copy
             first = unit_first(v)
+            rows = w_raw[(gate, v // UNITS_PER_STAGE)][:, :, first:first + UNIT]
+            if engine == "gpsimd":
+                nc.gpsimd.tensor_scalar(out=w_grp[(v, gate)][:], in0=rows.rearrange("p t n -> p n t"), scalar1=1.0,
+                                        scalar2=0.0, op0=ALU.mult, op1=ALU.add)
+                return
+            copy = nc.scalar.copy if engine == "scalar" else nc.vector.tensor_copy
             copy(
-                out=w_grp[(v, gate)][:, lo:hi, :].rearrange("p (c i) t -> p c t i", i=8),
-                in_=w_raw[(gate, v // UNITS_PER_STAGE)][:, :, first + lo:first + hi].rearrange("p t (c i) -> p c t i", i=8),
+                out=w_grp[(v, gate)][:].rearrange("p (c i) t -> p c t i", i=8),
+                in_=rows.rearrange("p t (c i) -> p c t i", i=8),
             )
 
         def quantise(v, gate):
@@ -225,15 +225,15 @@ def tile_blockgrucell_pb_kernel(tc, y_dyn, deter, gru_W, gru_b, out):
         def reset_gate(v):
             if not first_time("reset", v):
                 return
-            chains[v] = chain_pool.tile([P, TILES, BATCH], F32, name="chain")
+            xs[v] = gate_pool.tile([P, TILES, BATCH], F32, name="x")
             for i in range(TILES):
-                nc.scalar.activation(out=chains[v][:, i, :], in_=z_bank[(v, R)][:, i, :], func=FUNC.Sigmoid,
+                nc.scalar.activation(out=xs[v][:, i, :], in_=z_bank[(v, R)][:, i, :], func=FUNC.Sigmoid,
                                      bias=bias_col(R, v, i), scale=1.0)
 
         def update_gate(v):
             if not live(v):
                 return
-            upds[v] = upd_pool.tile([P, TILES, BATCH], F32, name="upd")
+            upds[v] = gate_pool.tile([P, TILES, BATCH], F32, name="upd")
             for i in range(TILES):
                 nc.scalar.activation(out=upds[v][:, i, :], in_=z_bank[(v, U)][:, i, :], func=FUNC.Sigmoid,
                                      bias=bias_col(U, v, i), scale=1.0)
@@ -242,57 +242,57 @@ def tile_blockgrucell_pb_kernel(tc, y_dyn, deter, gru_W, gru_b, out):
             if not first_time("reset times c", v):
                 return
             for i in range(TILES):
-                nc.vector.scalar_tensor_tensor(out=chains[v][:, i, :], in0=z_bank[(v, C)][:, i, :],
-                                               scalar=bias_col(C, v, i), in1=chains[v][:, i, :],
+                nc.vector.scalar_tensor_tensor(out=xs[v][:, i, :], in0=z_bank[(v, C)][:, i, :],
+                                               scalar=bias_col(C, v, i), in1=xs[v][:, i, :],
                                                op0=ALU.add, op1=ALU.mult)
+
+        def x_transpose(v):
+            if not live(v):
+                return
+            x_bank[v] = z_psum.tile([P, HALVES, UNIT], F32, name="xt")
+            for h in range(HALVES):
+                for i in range(TILES):
+                    nc.tensor.transpose(x_bank[v][:, h, i * P:(i + 1) * P], xs[v][:, i, h * P:(h + 1) * P], ident_f32[:])
 
         def cand_tanh(v):
             if live(v):
-                nc.scalar.activation(out=chains[v][:], in_=chains[v][:], func=FUNC.Tanh)
+                cands[v] = gate_pool.tile([P, HALVES, UNIT], F32, name="cand")
+                nc.scalar.activation(out=cands[v][:], in_=x_bank[v][:], func=FUNC.Tanh)
 
-        def deter_transpose(v):
+        def cand_minus_deter(v):
             if not live(v):
                 return
-            det_t[v] = dt_psum.tile([P, TILES, BATCH], BF16, name="dtile")
+            diff_bank[v] = z_psum.tile([P, TILES, BATCH], F32, name="diff")
             first = unit_first(v)
             for i in range(TILES):
                 for h in range(HALVES):
-                    nc.tensor.transpose(det_t[v][:, i, h * P:(h + 1) * P],
-                                        det_sb[v // UNITS_PER_STAGE][:, h, first + i * P:first + (i + 1) * P],
-                                        ident_bf[:])
-
-        def minus_deter(v):
-            if live(v):
-                nc.vector.tensor_tensor(out=chains[v][:], in0=chains[v][:], in1=det_t[v][:], op=ALU.subtract)
-
-        def on_gpsimd(v):
-            return live(v) and v < GPSIMD_UNITS
+                    piece = diff_bank[v][:, i, h * P:(h + 1) * P]
+                    nc.tensor.matmul(out=piece, lhsT=det_sb[v // UNITS_PER_STAGE][:, h, first + i * P:first + (i + 1) * P],
+                                     rhs=minus_ident[:], start=True, stop=False)
+                    nc.tensor.matmul(out=piece, lhsT=cands[v][:, h, i * P:(i + 1) * P], rhs=ident_f32[:],
+                                     is_transpose=True, start=False, stop=True)
 
         def times_update(v):
             if live(v):
-                engine = nc.gpsimd if on_gpsimd(v) else nc.vector
-                engine.tensor_tensor(out=chains[v][:], in0=chains[v][:], in1=upds[v][:], op=ALU.mult)
+                es[v] = gate_pool.tile([P, TILES, BATCH], F32, name="e")
+                nc.vector.tensor_tensor(out=es[v][:], in0=diff_bank[v][:], in1=upds[v][:], op=ALU.mult)
 
-        def back_transpose(v):
+        def e_transpose(v):
             if not live(v):
                 return
-            e_t[v] = et_psum.tile([P, HALVES, UNIT], F32, name="et")
-            first = unit_first(v)
-            nc.tensor.matmul(out=e_t[v][:], lhsT=ident_bf[:], rhs=det_sb[v // UNITS_PER_STAGE][:, :, first:first + UNIT],
-                             start=True, stop=False)
+            e_bank[v] = e_psum.tile([P, HALVES, UNIT], F32, name="et")
             for h in range(HALVES):
                 for i in range(TILES):
-                    nc.tensor.matmul(out=e_t[v][:, h, i * P:(i + 1) * P], lhsT=chains[v][:, i, h * P:(h + 1) * P],
-                                     rhs=ident_f32[:], is_transpose=True, start=False,
-                                     stop=(h == HALVES - 1 and i == TILES - 1))
+                    nc.tensor.transpose(e_bank[v][:, h, i * P:(i + 1) * P], es[v][:, i, h * P:(h + 1) * P], ident_f32[:])
 
-        def copy_out(v):
+        def add_deter(v):
             if not live(v):
                 return
             s = v // UNITS_PER_STAGE
             if v % UNITS_PER_STAGE == 0:
                 o_sb[s] = osb_pool.tile([P, HALVES, CHUNK], F32, name="osb")
-            nc.scalar.copy(out=o_sb[s][:, :, unit_cols(v)], in_=e_t[v][:])
+            nc.vector.tensor_tensor(out=o_sb[s][:, :, unit_cols(v)], in0=e_bank[v][:], in1=det_sb[s][:, :, unit_cols(v)],
+                                    op=ALU.add)
 
         def store(v):
             if not live(v):
@@ -310,11 +310,9 @@ def tile_blockgrucell_pb_kernel(tc, y_dyn, deter, gru_W, gru_b, out):
         u_first = U * D // P
         for gate in GATES:
             y_transpose(block_of(gate, 0))
-            for v in range(UNITS_PER_STAGE):
-                regroup(v, gate, scalar=True)
+            regroup(1, gate, "scalar")
             y_copy_out(block_of(gate, 0))
-            for v in range(UNITS_PER_STAGE):
-                regroup(v, gate, scalar=False)
+            regroup(0, gate, "vector")
             if gate != R:
                 for v in range(UNITS_PER_STAGE):
                     quantise(v, gate - 1)
@@ -338,47 +336,38 @@ def tile_blockgrucell_pb_kernel(tc, y_dyn, deter, gru_W, gru_b, out):
         reset_gate(1)
         passes(0, U)
 
-        last_slot = UNITS + 3
+        last_slot = UNITS + 1
         for k in range(last_slot + 1):
             if k % UNITS_PER_STAGE == 0 and k // UNITS_PER_STAGE + STAGES_RESIDENT < STAGES:
                 load_stage(k // UNITS_PER_STAGE + STAGES_RESIDENT)
             blocks_to_transpose = new_blocks((k + 3) // UNITS_PER_STAGE) if (k + 3) % UNITS_PER_STAGE == 0 else []
             blocks_to_quantise = new_blocks((k + 2) // UNITS_PER_STAGE) if k % UNITS_PER_STAGE == 0 else []
 
-            if on_gpsimd(k - 3):
-                back_transpose(k - 3)
-            reset_gate(k)
-            for g in blocks_to_quantise:
-                if k > 0:
-                    y_copy_out(g)
-            for gate in GATES:
-                regroup(k + 2, gate, scalar=True)
-            cand_tanh(k - 1)
-            if k == UNITS:
-                copy_out(k - 4)
-            update_gate(k)
-
-            if k > 0:
-                for gate in GATES:
-                    quantise(k + 1, gate)
-            if not on_gpsimd(k - 2):
-                times_update(k - 2)
-            for gate in GATES:
-                regroup(k + 2, gate, scalar=False)
-            for g in blocks_to_quantise:
-                y_quantise(g)
-            reset_times_c(k)
-            minus_deter(k - 1)
-
-            if on_gpsimd(k - 2):
-                times_update(k - 2)
-            else:
-                back_transpose(k - 2)
+            x_transpose(k - 1)
+            e_transpose(k - 2)
             for g in blocks_to_transpose:
                 y_transpose(g)
+
+            reset_gate(k)
+            cand_tanh(k - 1)
+            update_gate(k)
+            regroup(k + 2, R, "scalar")
+            for g in blocks_to_transpose:
+                y_copy_out(g)
+
+            cand_minus_deter(k - 1)
+
+            regroup(k + 2, C, "vector")
+            for g in blocks_to_quantise:
+                y_quantise(g)
+            if k > 0:
+                for gate in (C, R, U):
+                    quantise(k + 1, gate)
+            regroup(k + 2, U, "gpsimd")
+            reset_times_c(k)
+            add_deter(k - 2)
+            times_update(k - 1)
+
             for gate in (R, U, C):
                 passes(k + 1, gate)
-            deter_transpose(k)
-            if k != UNITS - 1:
-                copy_out(k - 3)
-            store(k - 3)
+            store(k - 2)

@@ -27,6 +27,7 @@ STAGES = D // CHUNK
 UNIT = 256
 TILES = UNIT // P
 UNITS = D // UNIT
+ALL = (0, 1)
 UNITS_PER_STAGE = CHUNK // UNIT
 STAGES_RESIDENT = 4
 
@@ -58,7 +59,7 @@ def tile_blockgrucell_pb_kernel(tc, y_dyn, deter, gru_W, gru_b, out):
         gate_pool = ctx.enter_context(tc.tile_pool(name="gate", bufs=4))
         osb_pool = ctx.enter_context(tc.tile_pool(name="osb", bufs=3))
         z_psum = ctx.enter_context(tc.psum_pool(name="zps", bufs=1))
-        e_psum = ctx.enter_context(tc.psum_pool(name="eps", bufs=2))
+        e_psum = ctx.enter_context(tc.psum_pool(name="eps", bufs=1))
         ctx.enter_context(tc.manual_schedule())
 
         warm_in = const.tile([P, 1], F32, name="warm_in")
@@ -135,10 +136,11 @@ def tile_blockgrucell_pb_kernel(tc, y_dyn, deter, gru_W, gru_b, out):
             for gate in GATES:
                 first = ((gate * STAGES + s) % 3) * CHUNK
                 w_raw[(gate, s)] = wraw_pool.tile([P, PACK, CHUNK], BF16, name="wr")
-                nc.sync.dma_start(
-                    out=w_raw[(gate, s)][:],
-                    in_=gru_W[block_of(gate, s), :, first:first + CHUNK].rearrange("(p j) n -> p j n", j=PACK),
-                )
+                for u in range(2):
+                    nc.sync.dma_start(
+                        out=w_raw[(gate, s)][:, 2 * u:2 * u + 2, :],
+                        in_=gru_W[block_of(gate, s), u * 256:u * 256 + 256, first:first + CHUNK].rearrange("(p j) n -> p j n", j=2),
+                    )
                 if s == 0:
                     load_y(block_of(gate, s))
             if s > 0:
@@ -152,7 +154,7 @@ def tile_blockgrucell_pb_kernel(tc, y_dyn, deter, gru_W, gru_b, out):
         def y_transpose(g):
             y_bank[g] = z_psum.tile([P, 2, BATCH], F32, name="yt")
             for h in range(HALVES):
-                words = y_raw[g][:, h, :].bitcast(F32).rearrange("b (p w) -> b w p", w=2)
+                words = y_raw[g][:, h, :].bitcast(F32).rearrange("b (w p) -> b w p", w=2)
                 for w in range(2):
                     nc.tensor.transpose(y_bank[g][:, w, h * P:(h + 1) * P], words[:, w, :], ident_f32[:])
 
@@ -217,16 +219,33 @@ def tile_blockgrucell_pb_kernel(tc, y_dyn, deter, gru_W, gru_b, out):
                     stop=True,
                 )
 
+        def keep_clock(n):
+            if n == 0:
+                return
+            bank = z_psum.tile([P, TILES, BATCH], F32, name="idle")
+            for i in range(n):
+                nc.tensor.matmul_mx(out=bank[:, i % 2, :], lhsT=y_codes[:, 0, 0:P].bitcast(FP8X4), lhsT_scale=y_scales[:, 0, 0:P],
+                                    rhs=y_codes[:, 0, :].bitcast(FP8X4), rhs_scale=y_scales[:, 0, :], start=True, stop=True)
+
 
         def bias_col(gate, v, i):
             j = gate * (D // P) + v * TILES + i
             return bias[:, j:j + 1]
 
-        def reset_gate(v):
-            if not first_time("reset", v):
+        def span(tiles):
+            return slice(tiles[0], tiles[-1] + 1)
+
+        def cols(tiles):
+            return slice(tiles[0] * P, (tiles[-1] + 1) * P)
+
+        def reset_gate(v, tiles=ALL):
+            if not live(v):
                 return
-            xs[v] = gate_pool.tile([P, TILES, BATCH], F32, name="x")
-            for i in range(TILES):
+            if v not in xs:
+                xs[v] = gate_pool.tile([P, TILES, BATCH], F32, name="x")
+            for i in tiles:
+                if not first_time("reset", v, i):
+                    continue
                 nc.scalar.activation(out=xs[v][:, i, :], in_=z_bank[(v, R)][:, i, :], func=FUNC.Sigmoid,
                                      bias=bias_col(R, v, i), scale=1.0)
 
@@ -238,61 +257,80 @@ def tile_blockgrucell_pb_kernel(tc, y_dyn, deter, gru_W, gru_b, out):
                 nc.scalar.activation(out=upds[v][:, i, :], in_=z_bank[(v, U)][:, i, :], func=FUNC.Sigmoid,
                                      bias=bias_col(U, v, i), scale=1.0)
 
-        def reset_times_c(v):
-            if not first_time("reset times c", v):
-                return
-            for i in range(TILES):
+        def reset_times_c(v, tiles=ALL):
+            for i in tiles:
+                if not first_time("reset times c", v, i):
+                    continue
                 nc.vector.scalar_tensor_tensor(out=xs[v][:, i, :], in0=z_bank[(v, C)][:, i, :],
                                                scalar=bias_col(C, v, i), in1=xs[v][:, i, :],
                                                op0=ALU.add, op1=ALU.mult)
 
-        def x_transpose(v):
+        def x_transpose(v, tiles=ALL, tag="xt"):
             if not live(v):
                 return
-            x_bank[v] = z_psum.tile([P, HALVES, UNIT], F32, name="xt")
+            for i in tiles:
+                x_bank[(v, i)] = z_psum.tile([P, HALVES, UNIT], F32, name="xt", tag=tag) if i == tiles[0] else x_bank[(v, tiles[0])]
             for h in range(HALVES):
-                for i in range(TILES):
-                    nc.tensor.transpose(x_bank[v][:, h, i * P:(i + 1) * P], xs[v][:, i, h * P:(h + 1) * P], ident_f32[:])
+                for i in tiles:
+                    nc.tensor.transpose(x_bank[(v, i)][:, h, i * P:(i + 1) * P], xs[v][:, i, h * P:(h + 1) * P], ident_f32[:])
 
-        def cand_tanh(v):
+        def cand_tanh(v, tiles=ALL):
             if live(v):
-                cands[v] = gate_pool.tile([P, HALVES, UNIT], F32, name="cand")
-                nc.scalar.activation(out=cands[v][:], in_=x_bank[v][:], func=FUNC.Tanh)
+                if v not in cands:
+                    cands[v] = gate_pool.tile([P, HALVES, UNIT], F32, name="cand")
+                nc.scalar.activation(out=cands[v][:, :, cols(tiles)], in_=x_bank[(v, tiles[0])][:, :, cols(tiles)], func=FUNC.Tanh)
 
-        def cand_minus_deter(v):
+        def cand_minus_deter(v, tiles=ALL, tag="diff"):
             if not live(v):
                 return
-            diff_bank[v] = z_psum.tile([P, TILES, BATCH], F32, name="diff")
+            for i in tiles:
+                diff_bank[(v, i)] = z_psum.tile([P, TILES, BATCH], F32, name="diff", tag=tag) if i == tiles[0] else diff_bank[(v, tiles[0])]
             first = unit_first(v)
-            for i in range(TILES):
+            for i in tiles:
                 for h in range(HALVES):
-                    piece = diff_bank[v][:, i, h * P:(h + 1) * P]
+                    piece = diff_bank[(v, i)][:, i, h * P:(h + 1) * P]
                     nc.tensor.matmul(out=piece, lhsT=det_sb[v // UNITS_PER_STAGE][:, h, first + i * P:first + (i + 1) * P],
                                      rhs=minus_ident[:], start=True, stop=False)
                     nc.tensor.matmul(out=piece, lhsT=cands[v][:, h, i * P:(i + 1) * P], rhs=ident_f32[:],
                                      is_transpose=True, start=False, stop=True)
 
-        def times_update(v):
+        def times_update(v, tiles=ALL):
             if live(v):
-                es[v] = gate_pool.tile([P, TILES, BATCH], F32, name="e")
-                nc.vector.tensor_tensor(out=es[v][:], in0=diff_bank[v][:], in1=upds[v][:], op=ALU.mult)
+                if v not in es:
+                    es[v] = gate_pool.tile([P, TILES, BATCH], F32, name="e")
+                i = span(tiles)
+                nc.vector.tensor_tensor(out=es[v][:, i, :], in0=diff_bank[(v, tiles[0])][:, i, :], in1=upds[v][:, i, :], op=ALU.mult)
 
-        def e_transpose(v):
+        def e_transpose(v, tiles=ALL, tag=None):
             if not live(v):
                 return
-            e_bank[v] = e_psum.tile([P, HALVES, UNIT], F32, name="et")
+            for i in tiles:
+                if i == tiles[0]:
+                    pool = z_psum if tag else e_psum
+                    e_bank[(v, i)] = pool.tile([P, HALVES, UNIT], F32, name="et", tag=tag or "et")
+                else:
+                    e_bank[(v, i)] = e_bank[(v, tiles[0])]
             for h in range(HALVES):
-                for i in range(TILES):
-                    nc.tensor.transpose(e_bank[v][:, h, i * P:(i + 1) * P], es[v][:, i, h * P:(h + 1) * P], ident_f32[:])
+                for i in tiles:
+                    nc.tensor.transpose(e_bank[(v, i)][:, h, i * P:(i + 1) * P], es[v][:, i, h * P:(h + 1) * P], ident_f32[:])
 
-        def add_deter(v):
+        def out_cols(v, tiles):
+            return slice(unit_first(v) + tiles[0] * P, unit_first(v) + (tiles[-1] + 1) * P)
+
+        def add_deter(v, tiles=ALL):
             if not live(v):
                 return
             s = v // UNITS_PER_STAGE
-            if v % UNITS_PER_STAGE == 0:
+            if s not in o_sb:
                 o_sb[s] = osb_pool.tile([P, HALVES, CHUNK], F32, name="osb")
-            nc.vector.tensor_tensor(out=o_sb[s][:, :, unit_cols(v)], in0=e_bank[v][:], in1=det_sb[s][:, :, unit_cols(v)],
-                                    op=ALU.add)
+            nc.vector.tensor_tensor(out=o_sb[s][:, :, out_cols(v, tiles)], in0=e_bank[(v, tiles[0])][:, :, cols(tiles)],
+                                    in1=det_sb[s][:, :, out_cols(v, tiles)], op=ALU.add)
+
+        def store_tiles(v, tiles):
+            s = v // UNITS_PER_STAGE
+            n = len(tiles) * P
+            first = v * UNIT + tiles[0] * P
+            nc.sync.dma_start(out=out_view[:, :, first:first + n], in_=o_sb[s][:, :, out_cols(v, tiles)])
 
         def store(v):
             if not live(v):
@@ -331,43 +369,76 @@ def tile_blockgrucell_pb_kernel(tc, y_dyn, deter, gru_W, gru_b, out):
         for v in range(UNITS_PER_STAGE):
             quantise(v, U)
         reset_times_c(0)
-        for g in new_blocks(1):
-            y_copy_out(g)
-        reset_gate(1)
         passes(0, U)
 
-        last_slot = UNITS + 1
-        for k in range(last_slot + 1):
+        for k in range(15):
             if k % UNITS_PER_STAGE == 0 and k // UNITS_PER_STAGE + STAGES_RESIDENT < STAGES:
                 load_stage(k // UNITS_PER_STAGE + STAGES_RESIDENT)
             blocks_to_transpose = new_blocks((k + 3) // UNITS_PER_STAGE) if (k + 3) % UNITS_PER_STAGE == 0 else []
             blocks_to_quantise = new_blocks((k + 2) // UNITS_PER_STAGE) if k % UNITS_PER_STAGE == 0 else []
 
             x_transpose(k - 1)
+            keep_clock(2)
             e_transpose(k - 2)
             for g in blocks_to_transpose:
                 y_transpose(g)
-
             reset_gate(k)
             cand_tanh(k - 1)
-            update_gate(k)
+            if k > 0:
+                update_gate(k)
             regroup(k + 2, R, "scalar")
             for g in blocks_to_transpose:
                 y_copy_out(g)
-
-            cand_minus_deter(k - 1)
-
+            if k == 0:
+                for g in new_blocks(1):
+                    y_copy_out(g)
+            if k == 0:
+                update_gate(k)
             regroup(k + 2, C, "vector")
-            for g in blocks_to_quantise:
+            for g in new_blocks(1) if k == 1 else blocks_to_quantise if k > 1 else []:
                 y_quantise(g)
             if k > 0:
-                for gate in (C, R, U):
-                    quantise(k + 1, gate)
+                quantise(k + 1, C)
+            if k > 0:
+                quantise(k + 1, R)
+            if k > 0:
+                quantise(k + 1, U)
             regroup(k + 2, U, "gpsimd")
+            cand_minus_deter(k - 1)
             reset_times_c(k)
             add_deter(k - 2)
             times_update(k - 1)
-
-            for gate in (R, U, C):
-                passes(k + 1, gate)
+            passes(k + 1, R)
+            passes(k + 1, U)
+            passes(k + 1, C)
             store(k - 2)
+
+        x_transpose(14)
+        keep_clock(2)
+        e_transpose(13)
+        reset_gate(15)
+        cand_tanh(14)
+        update_gate(15)
+        reset_times_c(15)
+        cand_minus_deter(14)
+        x_transpose(15,(0,))
+        x_transpose(15,(1,),"z0")
+        add_deter(13)
+        store(13)
+        times_update(14)
+        keep_clock(2)
+        cand_tanh(15,(0,))
+        cand_tanh(15,(1,))
+        e_transpose(14)
+        cand_minus_deter(15,(0,))
+        cand_minus_deter(15,(1,),"z1")
+        add_deter(14)
+        store(14)
+        times_update(15,(0,))
+        times_update(15,(1,))
+        e_transpose(15,(0,))
+        e_transpose(15,(1,),"yt")
+        add_deter(15,(0,))
+        store_tiles(15,(0,))
+        add_deter(15,(1,))
+        store_tiles(15,(1,))

@@ -370,6 +370,7 @@ def tile_blockgrucell_pb_kernel(tc, y_dyn, deter, gru_W, gru_b, out):
             quantise(v, U)
         reset_times_c(0)
         passes(0, U)
+        x_transpose(0)
 
         for k in range(15):
             if k % UNITS_PER_STAGE == 0 and k // UNITS_PER_STAGE + STAGES_RESIDENT < STAGES:
@@ -377,8 +378,9 @@ def tile_blockgrucell_pb_kernel(tc, y_dyn, deter, gru_W, gru_b, out):
             blocks_to_transpose = new_blocks((k + 3) // UNITS_PER_STAGE) if (k + 3) % UNITS_PER_STAGE == 0 else []
             blocks_to_quantise = new_blocks((k + 2) // UNITS_PER_STAGE) if k % UNITS_PER_STAGE == 0 else []
 
-            x_transpose(k - 1)
-            keep_clock(2)
+            if k > 1:
+                x_transpose(k - 1)
+            keep_clock(2 if k > 0 else 0)
             e_transpose(k - 2)
             for g in blocks_to_transpose:
                 y_transpose(g)
@@ -395,21 +397,24 @@ def tile_blockgrucell_pb_kernel(tc, y_dyn, deter, gru_W, gru_b, out):
             if k == 0:
                 update_gate(k)
             regroup(k + 2, C, "vector")
+            if k == 0:
+                regroup(k + 2, U, "vector")
             for g in new_blocks(1) if k == 1 else blocks_to_quantise if k > 1 else []:
                 y_quantise(g)
             if k > 0:
                 quantise(k + 1, C)
             if k > 0:
+                quantise(k + 1, U)
+            if k > 0:
                 quantise(k + 1, R)
             if k > 0:
-                quantise(k + 1, U)
-            regroup(k + 2, U, "gpsimd")
+                regroup(k + 2, U, "gpsimd")
             cand_minus_deter(k - 1)
             reset_times_c(k)
             add_deter(k - 2)
             times_update(k - 1)
-            passes(k + 1, R)
             passes(k + 1, U)
+            passes(k + 1, R)
             passes(k + 1, C)
             store(k - 2)
 

@@ -283,16 +283,24 @@ def tile_blockgrucell_pb_kernel(tc, y_dyn, deter, gru_W, gru_b, out):
         def cand_minus_deter(v, tiles=ALL, tag="diff"):
             if not live(v):
                 return
-            for i in tiles:
-                diff_bank[(v, i)] = z_psum.tile([P, TILES, BATCH], F32, name="diff", tag=tag) if i == tiles[0] else diff_bank[(v, tiles[0])]
-            first = unit_first(v)
+            if (v, tiles[0]) not in diff_bank:
+                minus_deter(v, tiles, tag)
             for i in tiles:
                 for h in range(HALVES):
-                    piece = diff_bank[(v, i)][:, i, h * P:(h + 1) * P]
-                    nc.tensor.matmul(out=piece, lhsT=det_sb[v // UNITS_PER_STAGE][:, h, first + i * P:first + (i + 1) * P],
-                                     rhs=minus_ident[:], start=True, stop=False)
-                    nc.tensor.matmul(out=piece, lhsT=cands[v][:, h, i * P:(i + 1) * P], rhs=ident_f32[:],
-                                     is_transpose=True, start=False, stop=True)
+                    nc.tensor.matmul(out=diff_bank[(v, i)][:, i, h * P:(h + 1) * P], lhsT=cands[v][:, h, i * P:(i + 1) * P],
+                                     rhs=ident_f32[:], is_transpose=True, start=False,
+                                     stop=(i == tiles[-1] and h == HALVES - 1))
+
+        def minus_deter(v, tiles=ALL, tag="diff"):
+            if not live(v):
+                return
+            first = unit_first(v)
+            for i in tiles:
+                diff_bank[(v, i)] = z_psum.tile([P, TILES, BATCH], F32, name="diff", tag=tag) if i == tiles[0] else diff_bank[(v, tiles[0])]
+                for h in range(HALVES):
+                    nc.tensor.matmul(out=diff_bank[(v, i)][:, i, h * P:(h + 1) * P],
+                                     lhsT=det_sb[v // UNITS_PER_STAGE][:, h, first + i * P:first + (i + 1) * P],
+                                     rhs=minus_ident[:], start=(i == tiles[0] and h == 0), stop=False)
 
         def times_update(v, tiles=ALL):
             if live(v):
@@ -384,6 +392,7 @@ def tile_blockgrucell_pb_kernel(tc, y_dyn, deter, gru_W, gru_b, out):
             e_transpose(k - 2)
             for g in blocks_to_transpose:
                 y_transpose(g)
+            minus_deter(k - 1)
             reset_gate(k)
             cand_tanh(k - 1)
             if k > 0:
@@ -421,6 +430,7 @@ def tile_blockgrucell_pb_kernel(tc, y_dyn, deter, gru_W, gru_b, out):
         x_transpose(14)
         keep_clock(2)
         e_transpose(13)
+        minus_deter(14)
         reset_gate(15)
         cand_tanh(14)
         update_gate(15)

@@ -389,10 +389,10 @@ def tile_blockgrucell_pb_kernel(tc, y_dyn, deter, gru_W, gru_b, out):
             if k > 1:
                 x_transpose(k - 1)
             keep_clock(2 if k > 0 else 0)
+            minus_deter(k - 1)
             e_transpose(k - 2)
             for g in blocks_to_transpose:
                 y_transpose(g)
-            minus_deter(k - 1)
             reset_gate(k)
             cand_tanh(k - 1)
             if k > 0:

@@ -57,7 +57,7 @@ def tile_blockgrucell_pb_kernel(tc, y_dyn, deter, gru_W, gru_b, out):
         wq_pool = ctx.enter_context(tc.tile_pool(name="wq", bufs=3))
         det_pool = ctx.enter_context(tc.tile_pool(name="det", bufs=STAGES))
         gate_pool = ctx.enter_context(tc.tile_pool(name="gate", bufs=4))
-        osb_pool = ctx.enter_context(tc.tile_pool(name="osb", bufs=3))
+        osb_pool = ctx.enter_context(tc.tile_pool(name="osb", bufs=4))
         z_psum = ctx.enter_context(tc.psum_pool(name="zps", bufs=1))
         e_psum = ctx.enter_context(tc.psum_pool(name="eps", bufs=1))
         ctx.enter_context(tc.manual_schedule())
@@ -170,22 +170,24 @@ def tile_blockgrucell_pb_kernel(tc, y_dyn, deter, gru_W, gru_b, out):
             )
 
 
-        def regroup(v, gate, engine):
+        def regroup(v, gate, engine, lo=0, hi=UNIT):
             if not live(v):
                 return
-            if gate == U and v >= UNITS_PER_STAGE:
+            if (v, gate) in w_grp:
+                pass
+            elif gate == U and v >= UNITS_PER_STAGE:
                 w_grp[(v, gate)] = wgrp_u_pool.tile([P, UNIT, PACK], BF16, name="wgu", align_bytes=64)
             else:
                 w_grp[(v, gate)] = wgrp_pool.tile([P, UNIT, PACK], BF16, name="wg%d" % gate, align_bytes=64)
             first = unit_first(v)
-            rows = w_raw[(gate, v // UNITS_PER_STAGE)][:, :, first:first + UNIT]
+            rows = w_raw[(gate, v // UNITS_PER_STAGE)][:, :, first + lo:first + hi]
             if engine == "gpsimd":
-                nc.gpsimd.tensor_scalar(out=w_grp[(v, gate)][:], in0=rows.rearrange("p t n -> p n t"), scalar1=1.0,
+                nc.gpsimd.tensor_scalar(out=w_grp[(v, gate)][:, lo:hi, :], in0=rows.rearrange("p t n -> p n t"), scalar1=1.0,
                                         scalar2=0.0, op0=ALU.mult, op1=ALU.add)
                 return
             copy = nc.scalar.copy if engine == "scalar" else nc.vector.tensor_copy
             copy(
-                out=w_grp[(v, gate)][:].rearrange("p (c i) t -> p c t i", i=8),
+                out=w_grp[(v, gate)][:, lo:hi, :].rearrange("p (c i) t -> p c t i", i=8),
                 in_=rows.rearrange("p t (c i) -> p c t i", i=8),
             )
 
@@ -398,6 +400,7 @@ def tile_blockgrucell_pb_kernel(tc, y_dyn, deter, gru_W, gru_b, out):
             if k > 0:
                 update_gate(k)
             regroup(k + 2, R, "scalar")
+            regroup(k + 2, C, "scalar", 0, 32)
             for g in blocks_to_transpose:
                 y_copy_out(g)
             if k == 0:
@@ -405,7 +408,7 @@ def tile_blockgrucell_pb_kernel(tc, y_dyn, deter, gru_W, gru_b, out):
                     y_copy_out(g)
             if k == 0:
                 update_gate(k)
-            regroup(k + 2, C, "vector")
+            regroup(k + 2, C, "vector", 32, UNIT)
             if k == 0:
                 regroup(k + 2, U, "vector")
             for g in new_blocks(1) if k == 1 else blocks_to_quantise if k > 1 else []:

@@ -59,7 +59,7 @@ def tile_blockgrucell_pb_kernel(tc, y_dyn, deter, gru_W, gru_b, out):
         gate_pool = ctx.enter_context(tc.tile_pool(name="gate", bufs=4))
         osb_pool = ctx.enter_context(tc.tile_pool(name="osb", bufs=4))
         z_psum = ctx.enter_context(tc.psum_pool(name="zps", bufs=1))
-        e_psum = ctx.enter_context(tc.psum_pool(name="eps", bufs=1))
+        e_psum = ctx.enter_context(tc.psum_pool(name="eps", bufs=2))
         ctx.enter_context(tc.manual_schedule())
 
         warm_in = const.tile([P, 1], F32, name="warm_in")
@@ -221,14 +221,6 @@ def tile_blockgrucell_pb_kernel(tc, y_dyn, deter, gru_W, gru_b, out):
                     stop=True,
                 )
 
-        def keep_clock(n):
-            if n == 0:
-                return
-            bank = z_psum.tile([P, TILES, BATCH], F32, name="idle")
-            for i in range(n):
-                nc.tensor.matmul_mx(out=bank[:, i % 2, :], lhsT=y_codes[:, 0, 0:P].bitcast(FP8X4), lhsT_scale=y_scales[:, 0, 0:P],
-                                    rhs=y_codes[:, 0, :].bitcast(FP8X4), rhs_scale=y_scales[:, 0, :], start=True, stop=True)
-
 
         def bias_col(gate, v, i):
             j = gate * (D // P) + v * TILES + i
@@ -378,6 +370,7 @@ def tile_blockgrucell_pb_kernel(tc, y_dyn, deter, gru_W, gru_b, out):
         passes(1, R)
         for v in range(UNITS_PER_STAGE):
             quantise(v, U)
+        regroup(2, R, "scalar")
         reset_times_c(0)
         passes(0, U)
         x_transpose(0)
@@ -390,73 +383,73 @@ def tile_blockgrucell_pb_kernel(tc, y_dyn, deter, gru_W, gru_b, out):
 
             if k > 1:
                 x_transpose(k - 1)
-            keep_clock(2 if k > 0 else 0)
+            reset_gate(k)
+            passes(k + 1, R)
             minus_deter(k - 1)
             e_transpose(k - 2)
             for g in blocks_to_transpose:
                 y_transpose(g)
-            reset_gate(k)
+
             cand_tanh(k - 1)
             if k > 0:
                 update_gate(k)
-            regroup(k + 2, R, "scalar")
             regroup(k + 2, C, "scalar", 0, 32)
-            for g in blocks_to_transpose:
-                y_copy_out(g)
             if k == 0:
                 for g in new_blocks(1):
                     y_copy_out(g)
+            regroup(k + 3, R, "scalar")
+            for g in blocks_to_transpose:
+                y_copy_out(g)
             if k == 0:
                 update_gate(k)
+
+            cand_minus_deter(k - 1)
+
             regroup(k + 2, C, "vector", 32, UNIT)
             if k == 0:
                 regroup(k + 2, U, "vector")
             for g in new_blocks(1) if k == 1 else blocks_to_quantise if k > 1 else []:
                 y_quantise(g)
             if k > 0:
-                quantise(k + 1, C)
-            if k > 0:
-                quantise(k + 1, U)
-            if k > 0:
-                quantise(k + 1, R)
+                for gate in (C, U):
+                    quantise(k + 1, gate)
+            quantise(k + 2, R)
             if k > 0:
                 regroup(k + 2, U, "gpsimd")
-            cand_minus_deter(k - 1)
             reset_times_c(k)
             add_deter(k - 2)
             times_update(k - 1)
             passes(k + 1, U)
-            passes(k + 1, R)
             passes(k + 1, C)
             store(k - 2)
 
         x_transpose(14)
-        keep_clock(2)
-        e_transpose(13)
-        minus_deter(14)
         reset_gate(15)
         cand_tanh(14)
         update_gate(15)
         reset_times_c(15)
+        minus_deter(14)
+        e_transpose(13)
         cand_minus_deter(14)
-        x_transpose(15,(0,))
-        x_transpose(15,(1,),"z0")
+        x_transpose(15, (0,), "z0")
+        x_transpose(15, (1,), "z1")
         add_deter(13)
         store(13)
         times_update(14)
-        keep_clock(2)
-        cand_tanh(15,(0,))
-        cand_tanh(15,(1,))
+        minus_deter(15, (0,), "z2")
+        minus_deter(15, (1,), "yt")
+        cand_tanh(15, (0,))
+        cand_tanh(15, (1,))
         e_transpose(14)
-        cand_minus_deter(15,(0,))
-        cand_minus_deter(15,(1,),"z1")
+        cand_minus_deter(15, (0,))
+        cand_minus_deter(15, (1,))
         add_deter(14)
         store(14)
-        times_update(15,(0,))
-        times_update(15,(1,))
-        e_transpose(15,(0,))
-        e_transpose(15,(1,),"yt")
-        add_deter(15,(0,))
-        store_tiles(15,(0,))
-        add_deter(15,(1,))
-        store_tiles(15,(1,))
+        times_update(15, (0,))
+        times_update(15, (1,))
+        e_transpose(15, (0,), "z0")
+        e_transpose(15, (1,), "z1")
+        add_deter(15, (0,))
+        store_tiles(15, (0,))
+        add_deter(15, (1,))
+        store_tiles(15, (1,))

@@ -397,7 +397,10 @@ def tile_blockgrucell_pb_kernel(tc, y_dyn, deter, gru_W, gru_b, out):
             if k == 0:
                 for g in new_blocks(1):
                     y_copy_out(g)
-            regroup(k + 3, R, "scalar")
+            if k > 0:
+                regroup(k + 3, R, "scalar")
+            else:
+                regroup(3, R, "gpsimd")
             for g in blocks_to_transpose:
                 y_copy_out(g)
             if k == 0:

from contextlib import ExitStack

import concourse.mybir as mybir
from concourse.masks import make_identity

F32 = mybir.dt.float32
BF16 = mybir.dt.bfloat16
U32 = mybir.dt.uint32
U8 = mybir.dt.uint8
FP8X4 = mybir.dt.float8_e4m3fn_x4
FUNC = mybir.ActivationFunctionType
ALU = mybir.AluOpType

P = 128
BATCH = 256
HALVES = BATCH // P
D = 4096
K = 512
BLOCKS = D // K
PACK = 4
R = 0
C = 1
U = 2
GATES = (R, C, U)
CHUNK = 512
STAGES = D // CHUNK
UNIT = 256
TILES = UNIT // P
UNITS = D // UNIT
ALL = (0, 1)
UNITS_PER_STAGE = CHUNK // UNIT
STAGES_RESIDENT = 4

FLOPS = 2 * BATCH * K * 3 * K * BLOCKS


def block_of(gate, stage):
    return (gate * STAGES + stage) // 3


def new_blocks(stage):
    if not 0 <= stage < STAGES:
        return []
    seen = [block_of(gate, s) for s in range(stage) for gate in GATES]
    return [block_of(gate, stage) for gate in GATES if block_of(gate, stage) not in seen]


def tile_blockgrucell_pb_kernel(tc, y_dyn, deter, gru_W, gru_b, out):
    nc = tc.nc
    with ExitStack() as ctx:
        const = ctx.enter_context(tc.tile_pool(name="const", bufs=1))
        yraw_pool = ctx.enter_context(tc.tile_pool(name="yraw", bufs=BLOCKS))
        ygrp_pool = ctx.enter_context(tc.tile_pool(name="ygrp", bufs=2))
        wraw_pool = ctx.enter_context(tc.tile_pool(name="wraw", bufs=len(GATES) * STAGES_RESIDENT))
        wgrp_pool = ctx.enter_context(tc.tile_pool(name="wgrp", bufs=3))
        wgrp_u_pool = ctx.enter_context(tc.tile_pool(name="wgrpu", bufs=1))
        wq_pool = ctx.enter_context(tc.tile_pool(name="wq", bufs=3))
        det_pool = ctx.enter_context(tc.tile_pool(name="det", bufs=STAGES))
        gate_pool = ctx.enter_context(tc.tile_pool(name="gate", bufs=4))
        osb_pool = ctx.enter_context(tc.tile_pool(name="osb", bufs=4))
        z_psum = ctx.enter_context(tc.psum_pool(name="zps", bufs=1))
        e_psum = ctx.enter_context(tc.psum_pool(name="eps", bufs=2))
        ctx.enter_context(tc.manual_schedule())

        warm_in = const.tile([P, 1], F32, name="warm_in")
        warm_out = const.tile([P, 1], F32, name="warm_out")
        nc.vector.memset(warm_in[:], 0.0)
        nc.scalar.activation(out=warm_out[:], in_=warm_in[:], func=FUNC.Sigmoid)

        ident_bf = const.tile([P, P], BF16, name="ident_bf")
        make_identity(nc, ident_bf[:])
        ident_f32 = const.tile([P, P], F32, name="ident_f32")
        make_identity(nc, ident_f32[:])
        minus_ident = const.tile([P, P], BF16, name="minus_ident")
        nc.vector.tensor_scalar_mul(out=minus_ident[:], in0=ident_bf[:], scalar1=-1.0)

        y_codes = const.tile([P, BLOCKS, BATCH], U32, name="y_codes", align_bytes=64)
        y_scales = const.tile([P, BLOCKS, BATCH], U8, name="y_scales", align_bytes=64)

        bias_cols = len(GATES) * D // P
        b_rows = const.tile([P, P], BF16, name="b_rows")
        nc.vector.memset(b_rows[bias_cols:P, :], 0.0)
        b_view = gru_b.rearrange("(j p) -> j p", p=P)
        nc.sync.dma_start(out=b_rows[0:64, :], in_=b_view[0:64, :])
        nc.sync.dma_start(out=b_rows[64:bias_cols, :], in_=b_view[64:bias_cols, :])
        bias = const.tile([P, bias_cols], F32, name="bias")

        y_view = y_dyn.rearrange("(h b) k -> b h k", h=HALVES)
        det_view = deter.rearrange("(h b) n -> b h n", h=HALVES)
        out_view = out.rearrange("(h b) n -> b h n", h=HALVES)

        w_raw = {}
        y_raw = {}
        y_bank = {}
        y_grp = {}
        det_sb = {}
        w_grp = {}
        w_q = {}
        z_bank = {}
        xs = {}
        x_bank = {}
        cands = {}
        upds = {}
        diff_bank = {}
        es = {}
        e_bank = {}
        o_sb = {}

        issued = set()

        def live(v):
            return 0 <= v < UNITS

        def first_time(what, v, gate=None):
            if not live(v) or (what, v, gate) in issued:
                return False
            issued.add((what, v, gate))
            return True

        def unit_first(v):
            return (v % UNITS_PER_STAGE) * UNIT

        def unit_cols(v):
            return slice(unit_first(v), unit_first(v) + UNIT)


        def load_y(g):
            y_raw[g] = yraw_pool.tile([P, HALVES, K], BF16, name="yr")
            nc.sync.dma_start(out=y_raw[g][:], in_=y_view[:, :, g * K:(g + 1) * K])

        def load_deter(s):
            det_sb[s] = det_pool.tile([P, HALVES, CHUNK], BF16, name="dsb")
            nc.sync.dma_start(out=det_sb[s][:], in_=det_view[:, :, s * CHUNK:(s + 1) * CHUNK])

        def load_stage(s):
            for gate in GATES:
                first = ((gate * STAGES + s) % 3) * CHUNK
                w_raw[(gate, s)] = wraw_pool.tile([P, PACK, CHUNK], BF16, name="wr")
                for u in range(2):
                    nc.sync.dma_start(
                        out=w_raw[(gate, s)][:, 2 * u:2 * u + 2, :],
                        in_=gru_W[block_of(gate, s), u * 256:u * 256 + 256, first:first + CHUNK].rearrange("(p j) n -> p j n", j=2),
                    )
                if s == 0:
                    load_y(block_of(gate, s))
            if s > 0:
                load_deter(s - 1)
            for g in new_blocks(s + 1):
                load_y(g)
            if s == STAGES - 1:
                load_deter(s)


        def y_transpose(g):
            y_bank[g] = z_psum.tile([P, 2, BATCH], F32, name="yt")
            for h in range(HALVES):
                words = y_raw[g][:, h, :].bitcast(F32).rearrange("b (w p) -> b w p", w=2)
                for w in range(2):
                    nc.tensor.transpose(y_bank[g][:, w, h * P:(h + 1) * P], words[:, w, :], ident_f32[:])

        def y_copy_out(g):
            y_grp[g] = ygrp_pool.tile([P, BATCH, PACK], BF16, name="yg", align_bytes=64)
            nc.scalar.copy(out=y_grp[g][:].bitcast(F32), in_=y_bank[g][:].rearrange("p w b -> p b w"))

        def y_quantise(g):
            nc.vector.quantize_mx(
                out=y_codes[:, g, :].bitcast(FP8X4),
                scales=y_scales[:, g, :],
                in_=y_grp[g][:].rearrange("p b t -> p (b t)"),
            )


        def regroup(v, gate, engine, lo=0, hi=UNIT):
            if not live(v):
                return
            if (v, gate) in w_grp:
                pass
            elif gate == U and v >= UNITS_PER_STAGE:
                w_grp[(v, gate)] = wgrp_u_pool.tile([P, UNIT, PACK], BF16, name="wgu", align_bytes=64)
            else:
                w_grp[(v, gate)] = wgrp_pool.tile([P, UNIT, PACK], BF16, name="wg%d" % gate, align_bytes=64)
            first = unit_first(v)
            rows = w_raw[(gate, v // UNITS_PER_STAGE)][:, :, first + lo:first + hi]
            if engine == "gpsimd":
                nc.gpsimd.tensor_scalar(out=w_grp[(v, gate)][:, lo:hi, :], in0=rows.rearrange("p t n -> p n t"), scalar1=1.0,
                                        scalar2=0.0, op0=ALU.mult, op1=ALU.add)
                return
            copy = nc.scalar.copy if engine == "scalar" else nc.vector.tensor_copy
            copy(
                out=w_grp[(v, gate)][:, lo:hi, :].rearrange("p (c i) t -> p c t i", i=8),
                in_=rows.rearrange("p t (c i) -> p c t i", i=8),
            )

        def quantise(v, gate):
            if not live(v):
                return
            codes = wq_pool.tile([P, UNIT], U32, name="codes%d" % gate, align_bytes=64)
            scales = wq_pool.tile([P, UNIT], U8, name="scales%d" % gate, align_bytes=64)
            nc.vector.quantize_mx(
                out=codes[:].bitcast(FP8X4),
                scales=scales[:],
                in_=w_grp[(v, gate)][:].rearrange("p n t -> p (n t)"),
            )
            w_q[(v, gate)] = (codes, scales)

        def passes(v, gate):
            if not first_time("passes", v, gate):
                return
            codes, scales = w_q[(v, gate)]
            g = block_of(gate, v // UNITS_PER_STAGE)
            z_bank[(v, gate)] = z_psum.tile([P, TILES, BATCH], F32, name="z%d" % gate)
            for i in range(TILES):
                cols = slice(i * P, (i + 1) * P)
                nc.tensor.matmul_mx(
                    out=z_bank[(v, gate)][:, i, :],
                    lhsT=codes[:, cols].bitcast(FP8X4),
                    lhsT_scale=scales[:, cols],
                    rhs=y_codes[:, g, :].bitcast(FP8X4),
                    rhs_scale=y_scales[:, g, :],
                    start=True,
                    stop=True,
                )


        def bias_col(gate, v, i):
            j = gate * (D // P) + v * TILES + i
            return bias[:, j:j + 1]

        def span(tiles):
            return slice(tiles[0], tiles[-1] + 1)

        def cols(tiles):
            return slice(tiles[0] * P, (tiles[-1] + 1) * P)

        def reset_gate(v, tiles=ALL):
            if not live(v):
                return
            if v not in xs:
                xs[v] = gate_pool.tile([P, TILES, BATCH], F32, name="x")
            for i in tiles:
                if not first_time("reset", v, i):
                    continue
                nc.scalar.activation(out=xs[v][:, i, :], in_=z_bank[(v, R)][:, i, :], func=FUNC.Sigmoid,
                                     bias=bias_col(R, v, i), scale=1.0)

        def update_gate(v):
            if not live(v):
                return
            upds[v] = gate_pool.tile([P, TILES, BATCH], F32, name="upd")
            for i in range(TILES):
                nc.scalar.activation(out=upds[v][:, i, :], in_=z_bank[(v, U)][:, i, :], func=FUNC.Sigmoid,
                                     bias=bias_col(U, v, i), scale=1.0)

        def reset_times_c(v, tiles=ALL):
            for i in tiles:
                if not first_time("reset times c", v, i):
                    continue
                nc.vector.scalar_tensor_tensor(out=xs[v][:, i, :], in0=z_bank[(v, C)][:, i, :],
                                               scalar=bias_col(C, v, i), in1=xs[v][:, i, :],
                                               op0=ALU.add, op1=ALU.mult)

        def x_transpose(v, tiles=ALL, tag="xt"):
            if not live(v):
                return
            for i in tiles:
                x_bank[(v, i)] = z_psum.tile([P, HALVES, UNIT], F32, name="xt", tag=tag) if i == tiles[0] else x_bank[(v, tiles[0])]
            for h in range(HALVES):
                for i in tiles:
                    nc.tensor.transpose(x_bank[(v, i)][:, h, i * P:(i + 1) * P], xs[v][:, i, h * P:(h + 1) * P], ident_f32[:])

        def cand_tanh(v, tiles=ALL):
            if live(v):
                if v not in cands:
                    cands[v] = gate_pool.tile([P, HALVES, UNIT], F32, name="cand")
                nc.scalar.activation(out=cands[v][:, :, cols(tiles)], in_=x_bank[(v, tiles[0])][:, :, cols(tiles)], func=FUNC.Tanh)

        def cand_minus_deter(v, tiles=ALL, tag="diff"):
            if not live(v):
                return
            if (v, tiles[0]) not in diff_bank:
                minus_deter(v, tiles, tag)
            for i in tiles:
                for h in range(HALVES):
                    nc.tensor.matmul(out=diff_bank[(v, i)][:, i, h * P:(h + 1) * P], lhsT=cands[v][:, h, i * P:(i + 1) * P],
                                     rhs=ident_f32[:], is_transpose=True, start=False,
                                     stop=(i == tiles[-1] and h == HALVES - 1))

        def minus_deter(v, tiles=ALL, tag="diff"):
            if not live(v):
                return
            first = unit_first(v)
            for i in tiles:
                diff_bank[(v, i)] = z_psum.tile([P, TILES, BATCH], F32, name="diff", tag=tag) if i == tiles[0] else diff_bank[(v, tiles[0])]
                for h in range(HALVES):
                    nc.tensor.matmul(out=diff_bank[(v, i)][:, i, h * P:(h + 1) * P],
                                     lhsT=det_sb[v // UNITS_PER_STAGE][:, h, first + i * P:first + (i + 1) * P],
                                     rhs=minus_ident[:], start=(i == tiles[0] and h == 0), stop=False)

        def times_update(v, tiles=ALL):
            if live(v):
                if v not in es:
                    es[v] = gate_pool.tile([P, TILES, BATCH], F32, name="e")
                i = span(tiles)
                nc.vector.tensor_tensor(out=es[v][:, i, :], in0=diff_bank[(v, tiles[0])][:, i, :], in1=upds[v][:, i, :], op=ALU.mult)

        def e_transpose(v, tiles=ALL, tag=None):
            if not live(v):
                return
            for i in tiles:
                if i == tiles[0]:
                    pool = z_psum if tag else e_psum
                    e_bank[(v, i)] = pool.tile([P, HALVES, UNIT], F32, name="et", tag=tag or "et")
                else:
                    e_bank[(v, i)] = e_bank[(v, tiles[0])]
            for h in range(HALVES):
                for i in tiles:
                    nc.tensor.transpose(e_bank[(v, i)][:, h, i * P:(i + 1) * P], es[v][:, i, h * P:(h + 1) * P], ident_f32[:])

        def out_cols(v, tiles):
            return slice(unit_first(v) + tiles[0] * P, unit_first(v) + (tiles[-1] + 1) * P)

        def add_deter(v, tiles=ALL):
            if not live(v):
                return
            s = v // UNITS_PER_STAGE
            if s not in o_sb:
                o_sb[s] = osb_pool.tile([P, HALVES, CHUNK], F32, name="osb")
            nc.vector.tensor_tensor(out=o_sb[s][:, :, out_cols(v, tiles)], in0=e_bank[(v, tiles[0])][:, :, cols(tiles)],
                                    in1=det_sb[s][:, :, out_cols(v, tiles)], op=ALU.add)

        def store_tiles(v, tiles):
            s = v // UNITS_PER_STAGE
            n = len(tiles) * P
            first = v * UNIT + tiles[0] * P
            nc.sync.dma_start(out=out_view[:, :, first:first + n], in_=o_sb[s][:, :, out_cols(v, tiles)])

        def store(v):
            if not live(v):
                return
            s = v // UNITS_PER_STAGE
            if s == STAGES - 1:
                nc.sync.dma_start(out=out_view[:, :, v * UNIT:(v + 1) * UNIT], in_=o_sb[s][:, :, unit_cols(v)])
            elif v % UNITS_PER_STAGE == UNITS_PER_STAGE - 1:
                nc.sync.dma_start(out=out_view[:, :, s * CHUNK:(s + 1) * CHUNK], in_=o_sb[s][:])


        for s in range(STAGES_RESIDENT):
            load_stage(s)

        u_first = U * D // P
        for gate in GATES:
            y_transpose(block_of(gate, 0))
            regroup(1, gate, "scalar")
            y_copy_out(block_of(gate, 0))
            regroup(0, gate, "vector")
            if gate != R:
                for v in range(UNITS_PER_STAGE):
                    quantise(v, gate - 1)
            if gate == C:
                bt = z_psum.tile([P, P], BF16, name="bt", tag="z%d" % U)
                nc.tensor.transpose(bt[:], b_rows[:], ident_bf[:])
                nc.vector.tensor_copy(out=bias[:, 0:u_first], in_=bt[:, 0:u_first])
                nc.vector.tensor_scalar_add(out=bias[:, u_first:bias_cols], in0=bt[:, u_first:bias_cols], scalar1=-1.0)
            y_quantise(block_of(gate, 0))
            if gate != R:
                passes(0, gate - 1)
        reset_gate(0)
        for g in new_blocks(1):
            y_transpose(g)
        passes(1, R)
        for v in range(UNITS_PER_STAGE):
            quantise(v, U)
        regroup(2, R, "scalar")
        reset_times_c(0)
        passes(0, U)
        x_transpose(0)

        for k in range(15):
            if k % UNITS_PER_STAGE == 0 and k // UNITS_PER_STAGE + STAGES_RESIDENT < STAGES:
                load_stage(k // UNITS_PER_STAGE + STAGES_RESIDENT)
            blocks_to_transpose = new_blocks((k + 3) // UNITS_PER_STAGE) if (k + 3) % UNITS_PER_STAGE == 0 else []
            blocks_to_quantise = new_blocks((k + 2) // UNITS_PER_STAGE) if k % UNITS_PER_STAGE == 0 else []

            if k > 1:
                x_transpose(k - 1)
            reset_gate(k)
            passes(k + 1, R)
            minus_deter(k - 1)
            e_transpose(k - 2)
            for g in blocks_to_transpose:
                y_transpose(g)

            cand_tanh(k - 1)
            if k > 0:
                update_gate(k)
            regroup(k + 2, C, "scalar", 0, 32)
            if k == 0:
                for g in new_blocks(1):
                    y_copy_out(g)
            if k > 0:
                regroup(k + 3, R, "scalar")
            else:
                regroup(3, R, "gpsimd")
            for g in blocks_to_transpose:
                y_copy_out(g)
            if k == 0:
                update_gate(k)

            cand_minus_deter(k - 1)

            regroup(k + 2, C, "vector", 32, UNIT)
            if k == 0:
                regroup(k + 2, U, "vector")
            for g in new_blocks(1) if k == 1 else blocks_to_quantise if k > 1 else []:
                y_quantise(g)
            if k > 0:
                for gate in (C, U):
                    quantise(k + 1, gate)
            quantise(k + 2, R)
            if k > 0:
                regroup(k + 2, U, "gpsimd")
            reset_times_c(k)
            add_deter(k - 2)
            times_update(k - 1)
            passes(k + 1, U)
            passes(k + 1, C)
            store(k - 2)

        x_transpose(14)
        reset_gate(15)
        cand_tanh(14)
        update_gate(15)
        reset_times_c(15)
        minus_deter(14)
        e_transpose(13)
        cand_minus_deter(14)
        x_transpose(15, (0,), "z0")
        x_transpose(15, (1,), "z1")
        add_deter(13)
        store(13)
        times_update(14)
        minus_deter(15, (0,), "z2")
        minus_deter(15, (1,), "yt")
        cand_tanh(15, (0,))
        cand_tanh(15, (1,))
        e_transpose(14)
        cand_minus_deter(15, (0,))
        cand_minus_deter(15, (1,))
        add_deter(14)
        store(14)
        times_update(15, (0,))
        times_update(15, (1,))
        e_transpose(15, (0,), "z0")
        e_transpose(15, (1,), "z1")
        add_deter(15, (0,))
        store_tiles(15, (0,))
        add_deter(15, (1,))
        store_tiles(15, (1,))
